import numpy as np
import ml_dtypes


def mxq(x, axis, fmt="e4m3"):
    dtype, down = {"e4m3": (ml_dtypes.float8_e4m3fn, 7), "e5m2": (ml_dtypes.float8_e5m2, 14)}[fmt]
    v = np.moveaxis(np.asarray(x, np.float32).astype(ml_dtypes.bfloat16).astype(np.float64), axis, -1)
    blocks = v.reshape(v.shape[:-1] + (-1, 32))
    amax = np.abs(blocks).max(-1, keepdims=True)
    byte = np.maximum(np.where(amax > 0, np.frexp(amax)[1] - 1 + 127, 0) - down, 1)
    scale = np.exp2(byte - 127.0)
    codes = (blocks / scale).astype(np.float32).astype(dtype).astype(np.float64)
    return np.moveaxis((codes * scale).reshape(v.shape), -1, axis)


WIDE = False


def mx_kscale(k):
    if not WIDE:
        return np.ones(k)
    levels = np.array([10, -10, 5, -5, 0])
    a = np.random.permutation(np.resize(levels, k // 512 * 4)).reshape(k // 512, 4)
    idx = np.arange(k)
    return np.exp2(a[idx // 512, idx % 128 // 32])


BF16 = ml_dtypes.bfloat16


def bf(x):
    return np.asarray(x, np.float32).astype(BF16)


def f64(x):
    return np.asarray(x).astype(np.float64)


E2M1 = np.array([0.0, 0.5, 1.0, 1.5, 2.0, 3.0, 4.0, 6.0, -0.0, -0.5, -1.0, -1.5, -2.0, -3.0, -4.0, -6.0])


def pack_weight(w, fmt):
    k, n = w.shape
    w = f64(bf(w)).reshape(k // 32, 32, n)
    amax = np.abs(w).max(1)
    if fmt == "e4m3":
        byte = np.frexp(amax)[1] - 1 + 127 - 7
    else:
        mant, ex = np.frexp(amax / 6.0)
        byte = np.where(mant > 0.5, ex, ex - 1) + 127
    byte = np.clip(np.where(amax > 0, byte, 1), 1, 254)
    scaled = (w * np.exp2(127.0 - byte)[:, None, :]).reshape(k, n).astype(np.float32)
    by_word = np.ascontiguousarray(scaled.reshape(k // 512, 128, 4, n).transpose(0, 1, 3, 2))
    if fmt == "e4m3":
        words = by_word.astype(ml_dtypes.float8_e4m3fn).view(np.uint8)
    else:
        c = by_word.astype(ml_dtypes.float4_e2m1fn).view(np.uint8) & 0xF
        words = c[..., 0::2] | (c[..., 1::2] << 4)
    return np.ascontiguousarray(words), np.ascontiguousarray(byte.astype(np.uint8).reshape(k // 512, 16, n))


def unpack_weight(words, scales, fmt):
    g, p, n, _ = words.shape
    if fmt == "e4m3":
        vals = np.ascontiguousarray(words).view(ml_dtypes.float8_e4m3fn).astype(np.float64)
    else:
        nib = np.empty((g, p, n, 4), np.uint8)
        nib[..., 0::2] = words & 0xF
        nib[..., 1::2] = words >> 4
        vals = E2M1[nib]
    vals = vals * np.repeat(np.exp2(scales.astype(np.float64) - 127.0), 8, axis=1)[..., None]
    return vals.transpose(0, 1, 3, 2).reshape(g * 512, n)


B, C, H, W, HS, WS = 4, 512, 32, 32, 16, 32
N = H * W
EPS = 1e-5


def mean_variance_norm(flat):
    mu = flat.mean(axis=-1, keepdims=True)
    sd = np.sqrt(flat.var(axis=-1, ddof=1, keepdims=True) + EPS)
    return (flat - mu) / sd


def setup_inputs():
    s = mx_kscale(C)
    gain = 0.7 + 0.6 * np.random.random_sample((B, C, 1, 1))
    shift = 0.4 * np.random.standard_normal((B, C, 1, 1))
    content = bf(np.random.standard_normal((B, C, H, W)) * gain + shift)
    mean = bf(np.random.standard_normal((B, C, H, W)) * 0.3 * s[:, None, None])
    std = bf(np.abs(1.0 + 0.25 * np.random.standard_normal((B, C, H, W))) * s[:, None, None])
    out_w = np.random.standard_normal((C, C)) / np.sqrt(C) / s
    words, scales = pack_weight(out_w.T, "e4m3")
    out_b = bf(np.random.standard_normal(C) * 0.2)
    return {"content": content,
            "mean": mean,
            "std": std,
            "out_w_words": words,
            "out_w_scales": scales,
            "out_b": out_b}


def reference(content, mean, std, out_w_words, out_w_scales, out_b):
    x = f64(content).reshape(B, C, N)
    o = f64(std).reshape(B, C, N) * mean_variance_norm(x) + f64(mean).reshape(B, C, N)
    y = (unpack_weight(out_w_words, out_w_scales, "e4m3").T @ mxq(o, 1, "e4m3")) + f64(out_b)[:, None]
    return (y + x).reshape(B, C, H, W)

@@ -1,0 +1,230 @@
+from contextlib import ExitStack
+
+import concourse.mybir as mybir
+from concourse.masks import make_identity
+
+F32 = mybir.dt.float32
+BF16 = mybir.dt.bfloat16
+I32 = mybir.dt.int32
+U32 = mybir.dt.uint32
+U8 = mybir.dt.uint8
+FP8X4 = mybir.dt.float8_e4m3fn_x4
+ALU = mybir.AluOpType
+ACT = mybir.ActivationFunctionType
+
+IMAGES = 4
+CHANNELS = 512
+PIXELS = 1024
+EPS = 1e-5
+P = 128
+PACK = 4
+M_TILES = CHANNELS // P
+N_TILE = 512
+HALVES = PIXELS // N_TILE
+UNITS = IMAGES * HALVES
+BN_CHUNK = 512
+BN_CHUNKS = PIXELS // BN_CHUNK
+BN_DIM = 6
+BLOCK_F32 = 8
+
+FLOPS = 2 * CHANNELS * CHANNELS * IMAGES * PIXELS
+
+VECTOR_ROWS = 6
+
+
+def tile_aattn_pb_t_kernel(tc, content, mean, std, out_w_words, out_w_scales, out_b, out):
+    nc = tc.nc
+    with ExitStack() as stack:
+        consts = stack.enter_context(tc.tile_pool(name="consts", bufs=1))
+        inputs = stack.enter_context(tc.tile_pool(name="inputs", bufs=1))
+        small = stack.enter_context(tc.tile_pool(name="small", bufs=1))
+        unread = stack.enter_context(tc.tile_pool(name="unread", bufs=4))
+        normed = stack.enter_context(tc.tile_pool(name="normed", bufs=2))
+        quant = stack.enter_context(tc.tile_pool(name="quant", bufs=2))
+        results = stack.enter_context(tc.tile_pool(name="results", bufs=8))
+        psum = stack.enter_context(tc.psum_pool(name="psum", bufs=8))
+        stack.enter_context(tc.manual_schedule())
+
+        def by_k(x, b):
+            return x[b].rearrange("(p t) h w -> p t (h w)", t=PACK)
+
+        def by_m(x, b):
+            return x[b].rearrange("(m j) h w -> j m (h w)", j=P)
+
+        def pixels_of(u):
+            h = u % HALVES
+            return slice(h * N_TILE, (h + 1) * N_TILE)
+
+        eps = consts.tile([P, 1], F32)
+        nc.vector.memset(eps[:], EPS)
+        warm = consts.tile([P, 1], F32)
+        nc.scalar.activation(out=warm[:], in_=eps[:], func=ACT.Sqrt)
+        bias_rows = consts.tile([P, P], BF16)
+        nc.vector.memset(bias_rows[:], 0.0)
+        nc.scalar.dma_start(out=bias_rows[0:M_TILES, :], in_=out_b.rearrange("(m j) -> m j", j=P))
+        w_plane = consts.tile([P, CHANNELS], U8, align_bytes=64)
+        nc.vector.memset(w_plane[:].bitcast(I32), 0)
+        ident = consts.tile([P, P], BF16)
+        make_identity(nc, ident[:])
+
+        x_k = [inputs.tile([P, PACK, PIXELS], BF16, name="x_k%d" % b) for b in range(IMAGES)]
+        std_k = [inputs.tile([P, PACK, PIXELS], BF16, name="std_k%d" % b) for b in range(IMAGES)]
+        mean_k = [inputs.tile([P, PACK, PIXELS], BF16, name="mean_k%d" % b) for b in range(IMAGES)]
+        x_m = [inputs.tile([P, M_TILES, PIXELS], BF16, name="x_m%d" % b) for b in range(IMAGES)]
+        w_codes = consts.tile([P, CHANNELS], U32, align_bytes=64)
+
+        for t in range(PACK):
+            nc.sync.dma_start(out=x_k[0][:, t, :], in_=by_k(content, 0)[:, t, :])
+        for b in range(IMAGES):
+            if b + 1 < IMAGES:
+                nc.sync.dma_start(out=x_k[b + 1][:], in_=by_k(content, b + 1))
+            nc.sync.dma_start(out=std_k[b][:], in_=by_k(std, b))
+            nc.sync.dma_start(out=mean_k[b][:], in_=by_k(mean, b))
+            if b == 0:
+                nc.sync.dma_start(
+                    out=w_codes[:].bitcast(I32),
+                    in_=out_w_words[0].rearrange("p n t -> p (n t)").bitcast(I32),
+                )
+                for q in range(4):
+                    nc.sync.dma_start(
+                        out=w_plane[32 * q : 32 * q + 4, :].bitcast(I32),
+                        in_=out_w_scales[0, 4 * q : 4 * q + 4, :].bitcast(I32),
+                    )
+            nc.sync.dma_start(out=x_m[b][:], in_=by_m(content, b))
+
+        mu_var = [small.tile([P, PACK, BLOCK_F32], F32, name="mu_var%d" % b) for b in range(IMAGES)]
+        spread = [small.tile([P, PACK], F32, name="spread%d" % b) for b in range(IMAGES)]
+        rstd = [small.tile([P, PACK], F32, name="rstd%d" % b) for b in range(IMAGES)]
+        shift = [small.tile([P, PACK], F32, name="shift%d" % b) for b in range(IMAGES)]
+        work = [None] * IMAGES
+
+        def vector_rows(b):
+            return max(0, min(PACK, VECTOR_ROWS - b * PACK))
+
+        def stats_on_vector(b):
+            parts = small.tile([P, PACK, BN_CHUNKS, BN_DIM], F32, name="parts%d" % b)
+            for t in range(vector_rows(b)):
+                for c in range(BN_CHUNKS):
+                    nc.vector.bn_stats(
+                        out=parts[:, t, c, :], in_=x_k[b][:, t, c * BN_CHUNK : (c + 1) * BN_CHUNK]
+                    )
+                nc.vector.bn_aggr(
+                    out=mu_var[b][:, t, 0:2], in_=parts[:, t].rearrange("p c s -> p (c s)")
+                )
+
+        def stats_on_scalar(b):
+            rows = range(vector_rows(b), PACK)
+            first = vector_rows(b)
+            if first < PACK:
+                total = small.tile([P, PACK], F32, name="total%d" % b)
+                squares = small.tile([P, PACK], F32, name="squares%d" % b)
+                for t in rows:
+                    copy_unread = unread.tile([P, PIXELS], BF16, tag="unread")
+                    nc.scalar.activation(
+                        out=copy_unread[:], in_=x_k[b][:, t, :], func=ACT.Identity,
+                        accum_out=total[:, t : t + 1],
+                    )
+                nc.scalar.mul(out=mu_var[b][:, first:, 0], in_=total[:, first:], mul=1.0 / PIXELS)
+                for t in rows:
+                    square_unread = unread.tile([P, PIXELS], BF16, tag="unread")
+                    nc.scalar.activation(
+                        out=square_unread[:], in_=x_k[b][:, t, :], func=ACT.Square,
+                        scale=-1.0, bias=mu_var[b][:, t, 0:1], accum_out=squares[:, t : t + 1],
+                    )
+                nc.scalar.mul(out=mu_var[b][:, first:, 1], in_=squares[:, first:], mul=1.0 / PIXELS)
+            nc.scalar.activation(
+                out=spread[b][:], in_=mu_var[b][:, :, 1], func=ACT.Sqrt,
+                scale=PIXELS / (PIXELS - 1.0), bias=eps[:],
+            )
+
+        def normalise(b):
+            nc.vector.reciprocal(out=rstd[b][:], in_=spread[b][:])
+            nc.vector.scalar_tensor_tensor(
+                out=shift[b][:], in0=mu_var[b][:, :, 0], scalar=-1.0, in1=rstd[b][:],
+                op0=ALU.mult, op1=ALU.mult,
+            )
+            work[b] = normed.tile([P, PACK, PIXELS], F32, name="work", tag="work")
+            for h in range(HALVES):
+                cols = pixels_of(h)
+                for t in range(PACK):
+                    nc.scalar.activation(
+                        out=work[b][:, t, cols], in_=x_k[b][:, t, cols], func=ACT.Identity,
+                        scale=rstd[b][:, t : t + 1], bias=shift[b][:, t : t + 1],
+                    )
+
+        grouped = [None] * UNITS
+        banks = [None] * UNITS
+
+        def multiply_by_std(u):
+            b, cols = u // HALVES, pixels_of(u)
+            nc.vector.tensor_tensor(
+                out=work[b][:, :, cols], in0=work[b][:, :, cols], in1=std_k[b][:, :, cols],
+                op=ALU.mult,
+            )
+
+        def add_mean(u):
+            b, cols = u // HALVES, pixels_of(u)
+            grouped[u] = quant.tile([P, N_TILE, PACK], BF16, align_bytes=64, name="grouped", tag="grouped")
+            nc.vector.tensor_tensor(
+                out=grouped[u][:],
+                in0=work[b][:, :, cols].rearrange("p t n -> p n t"),
+                in1=mean_k[b][:, :, cols].rearrange("p t n -> p n t"),
+                op=ALU.add,
+            )
+
+        def quantise_and_project(u):
+            o_codes = quant.tile([P, N_TILE], U32, align_bytes=64)
+            o_plane = quant.tile([P, N_TILE], U8, align_bytes=64)
+            nc.vector.quantize_mx(
+                out=o_codes[:].bitcast(FP8X4),
+                scales=o_plane[:],
+                in_=grouped[u][:].rearrange("p n t -> p (n t)"),
+            )
+            banks[u] = []
+            for m in range(M_TILES):
+                m_cols = slice(m * P, (m + 1) * P)
+                acc = psum.tile([P, N_TILE], F32, tag="acc")
+                nc.tensor.matmul_mx(
+                    out=acc[:],
+                    lhsT=w_codes[:, m_cols].bitcast(FP8X4),
+                    lhsT_scale=w_plane[:, m_cols],
+                    rhs=o_codes[:].bitcast(FP8X4),
+                    rhs_scale=o_plane[:],
+                    start=True,
+                    stop=True,
+                )
+                banks[u].append(acc)
+
+        def add_residual_and_store(u):
+            b, cols = u // HALVES, pixels_of(u)
+            for m in range(M_TILES):
+                result = results.tile([P, N_TILE], F32)
+                nc.vector.scalar_tensor_tensor(
+                    out=result[:], in0=banks[u][m][:], scalar=bias[:, m : m + 1],
+                    in1=x_m[b][:, m, cols], op0=ALU.add, op1=ALU.add,
+                )
+                nc.sync.dma_start(out=by_m(out, b)[:, m, cols], in_=result[:])
+
+        stats_on_vector(0)
+        stats_on_scalar(0)
+        normalise(0)
+        stats_on_vector(1)
+        stats_on_scalar(1)
+
+        bias_t = psum.tile([P, P], BF16, tag="acc")
+        nc.tensor.transpose(bias_t[:], bias_rows[:], ident[:])
+        bias = consts.tile([P, M_TILES], F32)
+        nc.vector.tensor_copy(out=bias[:], in_=bias_t[:, 0:M_TILES])
+
+        for u in range(UNITS + 1):
+            if u < UNITS:
+                multiply_by_std(u)
+                if u % HALVES == HALVES - 1 and u // HALVES + 1 < IMAGES:
+                    normalise(u // HALVES + 1)
+                    if u // HALVES + 2 < IMAGES:
+                        stats_on_scalar(u // HALVES + 2)
+                add_mean(u)
+            if u >= 1:
+                add_residual_and_store(u - 1)
+            if u < UNITS:
+                quantise_and_project(u)

@@ -30,6 +30,7 @@ BLOCK_F32 = 8
 FLOPS = 2 * CHANNELS * CHANNELS * IMAGES * PIXELS
 
 VECTOR_ROWS = 6
+RUN = 4
 
 
 def tile_aattn_pb_t_kernel(tc, content, mean, std, out_w_words, out_w_scales, out_b, out):
@@ -166,9 +167,9 @@ def tile_aattn_pb_t_kernel(tc, content, mean, std, out_w_words, out_w_scales, ou
             b, cols = u // HALVES, pixels_of(u)
             grouped[u] = quant.tile([P, N_TILE, PACK], BF16, align_bytes=64, name="grouped", tag="grouped")
             nc.vector.tensor_tensor(
-                out=grouped[u][:],
-                in0=work[b][:, :, cols].rearrange("p t n -> p n t"),
-                in1=mean_k[b][:, :, cols].rearrange("p t n -> p n t"),
+                out=grouped[u][:].rearrange("p (c i) t -> p c t i", i=RUN),
+                in0=work[b][:, :, cols].rearrange("p t (c i) -> p c t i", i=RUN),
+                in1=mean_k[b][:, :, cols].rearrange("p t (c i) -> p c t i", i=RUN),
                 op=ALU.add,
             )
 

@@ -42,7 +42,7 @@ def tile_aattn_pb_t_kernel(tc, content, mean, std, out_w_words, out_w_scales, ou
         unread = stack.enter_context(tc.tile_pool(name="unread", bufs=4))
         normed = stack.enter_context(tc.tile_pool(name="normed", bufs=2))
         quant = stack.enter_context(tc.tile_pool(name="quant", bufs=2))
-        results = stack.enter_context(tc.tile_pool(name="results", bufs=8))
+        results = stack.enter_context(tc.tile_pool(name="results", bufs=16))
         psum = stack.enter_context(tc.psum_pool(name="psum", bufs=8))
         stack.enter_context(tc.manual_schedule())
 
@@ -217,15 +217,17 @@ def tile_aattn_pb_t_kernel(tc, content, mean, std, out_w_words, out_w_scales, ou
         bias = consts.tile([P, M_TILES], F32)
         nc.vector.tensor_copy(out=bias[:], in_=bias_t[:, 0:M_TILES])
 
-        for u in range(UNITS + 1):
-            if u < UNITS:
-                multiply_by_std(u)
-                if u % HALVES == HALVES - 1 and u // HALVES + 1 < IMAGES:
-                    normalise(u // HALVES + 1)
-                    if u // HALVES + 2 < IMAGES:
-                        stats_on_scalar(u // HALVES + 2)
+        for b in range(IMAGES):
+            for h in range(HALVES):
+                multiply_by_std(b * HALVES + h)
+            for h in range(HALVES):
+                u = b * HALVES + h
+                if h == HALVES - 1 and b + 1 < IMAGES:
+                    normalise(b + 1)
+                    if b + 2 < IMAGES:
+                        stats_on_scalar(b + 2)
                 add_mean(u)
-            if u >= 1:
-                add_residual_and_store(u - 1)
-            if u < UNITS:
+                if u >= 1:
+                    add_residual_and_store(u - 1)
                 quantise_and_project(u)
+        add_residual_and_store(UNITS - 1)

@@ -31,6 +31,7 @@ FLOPS = 2 * CHANNELS * CHANNELS * IMAGES * PIXELS
 
 VECTOR_ROWS = 6
 RUN = 4
+GPSIMD_PIXELS = 160
 
 
 def tile_aattn_pb_t_kernel(tc, content, mean, std, out_w_words, out_w_scales, out_b, out):
@@ -52,9 +53,9 @@ def tile_aattn_pb_t_kernel(tc, content, mean, std, out_w_words, out_w_scales, ou
         def by_m(x, b):
             return x[b].rearrange("(m j) h w -> j m (h w)", j=P)
 
-        def pixels_of(u):
-            h = u % HALVES
-            return slice(h * N_TILE, (h + 1) * N_TILE)
+        def pixels_of(u, first=0, count=N_TILE):
+            start = (u % HALVES) * N_TILE + first
+            return slice(start, start + count)
 
         eps = consts.tile([P, 1], F32)
         nc.vector.memset(eps[:], EPS)
@@ -94,6 +95,8 @@ def tile_aattn_pb_t_kernel(tc, content, mean, std, out_w_words, out_w_scales, ou
             nc.sync.dma_start(out=x_m[b][:], in_=by_m(content, b))
 
         mu_var = [small.tile([P, PACK, BLOCK_F32], F32, name="mu_var%d" % b) for b in range(IMAGES)]
+        total = [None] * IMAGES
+        squares = [None] * IMAGES
         spread = [small.tile([P, PACK], F32, name="spread%d" % b) for b in range(IMAGES)]
         rstd = [small.tile([P, PACK], F32, name="rstd%d" % b) for b in range(IMAGES)]
         shift = [small.tile([P, PACK], F32, name="shift%d" % b) for b in range(IMAGES)]
@@ -113,26 +116,31 @@ def tile_aattn_pb_t_kernel(tc, content, mean, std, out_w_words, out_w_scales, ou
                     out=mu_var[b][:, t, 0:2], in_=parts[:, t].rearrange("p c s -> p (c s)")
                 )
 
-        def stats_on_scalar(b):
-            rows = range(vector_rows(b), PACK)
+        def means_on_scalar(b):
             first = vector_rows(b)
             if first < PACK:
-                total = small.tile([P, PACK], F32, name="total%d" % b)
-                squares = small.tile([P, PACK], F32, name="squares%d" % b)
-                for t in rows:
-                    copy_unread = unread.tile([P, PIXELS], BF16, tag="unread")
-                    nc.scalar.activation(
-                        out=copy_unread[:], in_=x_k[b][:, t, :], func=ACT.Identity,
-                        accum_out=total[:, t : t + 1],
-                    )
-                nc.scalar.mul(out=mu_var[b][:, first:, 0], in_=total[:, first:], mul=1.0 / PIXELS)
-                for t in rows:
-                    square_unread = unread.tile([P, PIXELS], BF16, tag="unread")
-                    nc.scalar.activation(
-                        out=square_unread[:], in_=x_k[b][:, t, :], func=ACT.Square,
-                        scale=-1.0, bias=mu_var[b][:, t, 0:1], accum_out=squares[:, t : t + 1],
-                    )
-                nc.scalar.mul(out=mu_var[b][:, first:, 1], in_=squares[:, first:], mul=1.0 / PIXELS)
+                total[b] = small.tile([P, PACK], F32, name="total%d" % b)
+            for t in range(first, PACK):
+                copy_unread = unread.tile([P, PIXELS], BF16, tag="unread")
+                nc.scalar.activation(
+                    out=copy_unread[:], in_=x_k[b][:, t, :], func=ACT.Identity,
+                    accum_out=total[b][:, t : t + 1],
+                )
+            if first < PACK:
+                nc.scalar.mul(out=mu_var[b][:, first:, 0], in_=total[b][:, first:], mul=1.0 / PIXELS)
+
+        def spreads_on_scalar(b):
+            first = vector_rows(b)
+            if first < PACK:
+                squares[b] = small.tile([P, PACK], F32, name="squares%d" % b)
+            for t in range(first, PACK):
+                square_unread = unread.tile([P, PIXELS], BF16, tag="unread")
+                nc.scalar.activation(
+                    out=square_unread[:], in_=x_k[b][:, t, :], func=ACT.Square,
+                    scale=-1.0, bias=mu_var[b][:, t, 0:1], accum_out=squares[b][:, t : t + 1],
+                )
+            if first < PACK:
+                nc.scalar.mul(out=mu_var[b][:, first:, 1], in_=squares[b][:, first:], mul=1.0 / PIXELS)
             nc.scalar.activation(
                 out=spread[b][:], in_=mu_var[b][:, :, 1], func=ACT.Sqrt,
                 scale=PIXELS / (PIXELS - 1.0), bias=eps[:],
@@ -156,20 +164,31 @@ def tile_aattn_pb_t_kernel(tc, content, mean, std, out_w_words, out_w_scales, ou
         grouped = [None] * UNITS
         banks = [None] * UNITS
 
-        def multiply_by_std(u):
-            b, cols = u // HALVES, pixels_of(u)
+        def gpsimd_pixels(u):
+            return GPSIMD_PIXELS if u > 0 else 0
+
+        def multiply_by_std_on_vector(u):
+            b, cols = u // HALVES, pixels_of(u, 0, N_TILE - gpsimd_pixels(u))
             nc.vector.tensor_tensor(
                 out=work[b][:, :, cols], in0=work[b][:, :, cols], in1=std_k[b][:, :, cols],
                 op=ALU.mult,
             )
 
-        def add_mean(u):
-            b, cols = u // HALVES, pixels_of(u)
-            grouped[u] = quant.tile([P, N_TILE, PACK], BF16, align_bytes=64, name="grouped", tag="grouped")
+        def multiply_by_std_on_gpsimd(u):
+            b, count = u // HALVES, gpsimd_pixels(u)
+            if count > 0:
+                last = pixels_of(u, N_TILE - count, count)
+                nc.gpsimd.tensor_tensor(
+                    out=work[b][:, :, pixels_of(u, 0, count)], in0=work[b][:, :, last],
+                    in1=std_k[b][:, :, last], op=ALU.mult,
+                )
+
+        def add_mean(u, first, count, product_first):
+            b = u // HALVES
             nc.vector.tensor_tensor(
-                out=grouped[u][:].rearrange("p (c i) t -> p c t i", i=RUN),
-                in0=work[b][:, :, cols].rearrange("p t (c i) -> p c t i", i=RUN),
-                in1=mean_k[b][:, :, cols].rearrange("p t (c i) -> p c t i", i=RUN),
+                out=grouped[u][:, first : first + count, :].rearrange("p (c i) t -> p c t i", i=RUN),
+                in0=work[b][:, :, pixels_of(u, product_first, count)].rearrange("p t (c i) -> p c t i", i=RUN),
+                in1=mean_k[b][:, :, pixels_of(u, first, count)].rearrange("p t (c i) -> p c t i", i=RUN),
                 op=ALU.add,
             )
 
@@ -207,27 +226,36 @@ def tile_aattn_pb_t_kernel(tc, content, mean, std, out_w_words, out_w_scales, ou
                 nc.sync.dma_start(out=by_m(out, b)[:, m, cols], in_=result[:])
 
         stats_on_vector(0)
-        stats_on_scalar(0)
+        spreads_on_scalar(0)
         normalise(0)
         stats_on_vector(1)
-        stats_on_scalar(1)
+        means_on_scalar(1)
+        spreads_on_scalar(1)
+        means_on_scalar(2)
 
         bias_t = psum.tile([P, P], BF16, tag="acc")
         nc.tensor.transpose(bias_t[:], bias_rows[:], ident[:])
         bias = consts.tile([P, M_TILES], F32)
         nc.vector.tensor_copy(out=bias[:], in_=bias_t[:, 0:M_TILES])
 
-        for b in range(IMAGES):
-            for h in range(HALVES):
-                multiply_by_std(b * HALVES + h)
-            for h in range(HALVES):
-                u = b * HALVES + h
-                if h == HALVES - 1 and b + 1 < IMAGES:
-                    normalise(b + 1)
-                    if b + 2 < IMAGES:
-                        stats_on_scalar(b + 2)
-                add_mean(u)
-                if u >= 1:
-                    add_residual_and_store(u - 1)
-                quantise_and_project(u)
+        multiply_by_std_on_vector(0)
+        for u in range(UNITS):
+            b = u // HALVES
+            if u % HALVES == HALVES - 1 and b + 1 < IMAGES:
+                normalise(b + 1)
+                if b + 2 < IMAGES:
+                    spreads_on_scalar(b + 2)
+                if b + 3 < IMAGES:
+                    means_on_scalar(b + 3)
+            grouped[u] = quant.tile([P, N_TILE, PACK], BF16, align_bytes=64, name="grouped", tag="grouped")
+            own = N_TILE - gpsimd_pixels(u)
+            add_mean(u, 0, own, 0)
+            multiply_by_std_on_gpsimd(u)
+            if u >= 1:
+                add_residual_and_store(u - 1)
+            if own < N_TILE:
+                add_mean(u, own, N_TILE - own, 0)
+            if u + 1 < UNITS:
+                multiply_by_std_on_vector(u + 1)
+            quantise_and_project(u)
         add_residual_and_store(UNITS - 1)

@@ -1,7 +1,6 @@
 from contextlib import ExitStack
 
 import concourse.mybir as mybir
-from concourse.masks import make_identity
 
 F32 = mybir.dt.float32
 BF16 = mybir.dt.bfloat16
@@ -50,9 +49,6 @@ def tile_aattn_pb_t_kernel(tc, content, mean, std, out_w_words, out_w_scales, ou
         def by_k(x, b):
             return x[b].rearrange("(p t) h w -> p t (h w)", t=PACK)
 
-        def by_m(x, b):
-            return x[b].rearrange("(m j) h w -> j m (h w)", j=P)
-
         def pixels_of(u, first=0, count=N_TILE):
             start = (u % HALVES) * N_TILE + first
             return slice(start, start + count)
@@ -61,19 +57,15 @@ def tile_aattn_pb_t_kernel(tc, content, mean, std, out_w_words, out_w_scales, ou
         nc.vector.memset(eps[:], EPS)
         warm = consts.tile([P, 1], F32)
         nc.scalar.activation(out=warm[:], in_=eps[:], func=ACT.Sqrt)
-        bias_rows = consts.tile([P, P], BF16)
-        nc.vector.memset(bias_rows[:], 0.0)
-        nc.scalar.dma_start(out=bias_rows[0:M_TILES, :], in_=out_b.rearrange("(m j) -> m j", j=P))
-        w_plane = consts.tile([P, CHANNELS], U8, align_bytes=64)
-        nc.vector.memset(w_plane[:].bitcast(I32), 0)
-        ident = consts.tile([P, P], BF16)
-        make_identity(nc, ident[:])
+        bias = consts.tile([P, PACK], BF16)
+        nc.scalar.dma_start(out=bias[:], in_=out_b.rearrange("(j t) -> j t", t=PACK))
+        w_plane_raw = consts.tile([P, CHANNELS], U8, align_bytes=64)
+        nc.vector.memset(w_plane_raw[:].bitcast(I32), 0)
 
         x_k = [inputs.tile([P, PACK, PIXELS], BF16, name="x_k%d" % b) for b in range(IMAGES)]
         std_k = [inputs.tile([P, PACK, PIXELS], BF16, name="std_k%d" % b) for b in range(IMAGES)]
         mean_k = [inputs.tile([P, PACK, PIXELS], BF16, name="mean_k%d" % b) for b in range(IMAGES)]
-        x_m = [inputs.tile([P, M_TILES, PIXELS], BF16, name="x_m%d" % b) for b in range(IMAGES)]
-        w_codes = consts.tile([P, CHANNELS], U32, align_bytes=64)
+        w_codes_raw = consts.tile([P, CHANNELS], U32, align_bytes=64)
 
         for t in range(PACK):
             nc.sync.dma_start(out=x_k[0][:, t, :], in_=by_k(content, 0)[:, t, :])
@@ -84,15 +76,25 @@ def tile_aattn_pb_t_kernel(tc, content, mean, std, out_w_words, out_w_scales, ou
             nc.sync.dma_start(out=mean_k[b][:], in_=by_k(mean, b))
             if b == 0:
                 nc.sync.dma_start(
-                    out=w_codes[:].bitcast(I32),
+                    out=w_codes_raw[:].bitcast(I32),
                     in_=out_w_words[0].rearrange("p n t -> p (n t)").bitcast(I32),
                 )
                 for q in range(4):
                     nc.sync.dma_start(
-                        out=w_plane[32 * q : 32 * q + 4, :].bitcast(I32),
+                        out=w_plane_raw[32 * q : 32 * q + 4, :].bitcast(I32),
                         in_=out_w_scales[0, 4 * q : 4 * q + 4, :].bitcast(I32),
                     )
-            nc.sync.dma_start(out=x_m[b][:], in_=by_m(content, b))
+
+        w_codes = consts.tile([P, CHANNELS], U32, align_bytes=64)
+        w_plane = consts.tile([P, CHANNELS], U8, align_bytes=64)
+        nc.gpsimd.tensor_copy(
+            out=w_codes[:].rearrange("p (t j) -> p t j", t=PACK),
+            in_=w_codes_raw[:].rearrange("p (j t) -> p t j", t=PACK),
+        )
+        nc.gpsimd.tensor_copy(
+            out=w_plane[:].rearrange("p (t j) -> p j t", t=PACK),
+            in_=w_plane_raw[:].rearrange("p (j t) -> p j t", t=PACK),
+        )
 
         mu_var = [small.tile([P, PACK, BLOCK_F32], F32, name="mu_var%d" % b) for b in range(IMAGES)]
         total = [None] * IMAGES
@@ -221,9 +223,9 @@ def tile_aattn_pb_t_kernel(tc, content, mean, std, out_w_words, out_w_scales, ou
                 result = results.tile([P, N_TILE], F32)
                 nc.vector.scalar_tensor_tensor(
                     out=result[:], in0=banks[u][m][:], scalar=bias[:, m : m + 1],
-                    in1=x_m[b][:, m, cols], op0=ALU.add, op1=ALU.add,
+                    in1=x_k[b][:, m, cols], op0=ALU.add, op1=ALU.add,
                 )
-                nc.sync.dma_start(out=by_m(out, b)[:, m, cols], in_=result[:])
+                nc.sync.dma_start(out=by_k(out, b)[:, m, cols], in_=result[:])
 
         stats_on_vector(0)
         spreads_on_scalar(0)
@@ -232,11 +234,6 @@ def tile_aattn_pb_t_kernel(tc, content, mean, std, out_w_words, out_w_scales, ou
         means_on_scalar(1)
         spreads_on_scalar(1)
         means_on_scalar(2)
-
-        bias_t = psum.tile([P, P], BF16, tag="acc")
-        nc.tensor.transpose(bias_t[:], bias_rows[:], ident[:])
-        bias = consts.tile([P, M_TILES], F32)
-        nc.vector.tensor_copy(out=bias[:], in_=bias_t[:, 0:M_TILES])
 
         multiply_by_std_on_vector(0)
         for u in range(UNITS):

@@ -17,7 +17,6 @@ PIXELS = 1024
 EPS = 1e-5
 P = 128
 PACK = 4
-M_TILES = CHANNELS // P
 N_TILE = 512
 HALVES = PIXELS // N_TILE
 UNITS = IMAGES * HALVES
@@ -28,9 +27,9 @@ BLOCK_F32 = 8
 
 FLOPS = 2 * CHANNELS * CHANNELS * IMAGES * PIXELS
 
-VECTOR_ROWS = 6
+VECTOR_ROWS = (3, 2, 2, 1)
 RUN = 4
-GPSIMD_PIXELS = 160
+GPSIMD_PIXELS = 224
 
 
 def tile_aattn_pb_t_kernel(tc, content, mean, std, out_w_words, out_w_scales, out_b, out):
@@ -40,7 +39,7 @@ def tile_aattn_pb_t_kernel(tc, content, mean, std, out_w_words, out_w_scales, ou
         inputs = stack.enter_context(tc.tile_pool(name="inputs", bufs=1))
         small = stack.enter_context(tc.tile_pool(name="small", bufs=1))
         unread = stack.enter_context(tc.tile_pool(name="unread", bufs=4))
-        normed = stack.enter_context(tc.tile_pool(name="normed", bufs=2))
+        normed = stack.enter_context(tc.tile_pool(name="normed", bufs=3))
         quant = stack.enter_context(tc.tile_pool(name="quant", bufs=2))
         results = stack.enter_context(tc.tile_pool(name="results", bufs=16))
         psum = stack.enter_context(tc.psum_pool(name="psum", bufs=8))
@@ -67,23 +66,36 @@ def tile_aattn_pb_t_kernel(tc, content, mean, std, out_w_words, out_w_scales, ou
         mean_k = [inputs.tile([P, PACK, PIXELS], BF16, name="mean_k%d" % b) for b in range(IMAGES)]
         w_codes_raw = consts.tile([P, CHANNELS], U32, align_bytes=64)
 
-        for t in range(PACK):
-            nc.sync.dma_start(out=x_k[0][:, t, :], in_=by_k(content, 0)[:, t, :])
-        for b in range(IMAGES):
-            if b + 1 < IMAGES:
-                nc.sync.dma_start(out=x_k[b + 1][:], in_=by_k(content, b + 1))
+        def load_rows(b, rows):
+            for t in rows:
+                nc.sync.dma_start(out=x_k[b][:, t, :], in_=by_k(content, b)[:, t, :])
+
+        def load_half(tiles, x, u):
+            b, cols = u // HALVES, pixels_of(u)
+            nc.sync.dma_start(out=tiles[b][:, :, cols], in_=by_k(x, b)[:, :, cols])
+
+        load_rows(0, range(PACK))
+        nc.sync.dma_start(
+            out=w_codes_raw[:].bitcast(I32),
+            in_=out_w_words[0].rearrange("p n t -> p (n t)").bitcast(I32),
+        )
+        for q in range(4):
+            nc.sync.dma_start(
+                out=w_plane_raw[32 * q : 32 * q + 4, :].bitcast(I32),
+                in_=out_w_scales[0, 4 * q : 4 * q + 4, :].bitcast(I32),
+            )
+        load_rows(1, range(PACK))
+        load_half(std_k, std, 0)
+        load_half(mean_k, mean, 0)
+        load_half(std_k, std, 1)
+        load_rows(2, range(VECTOR_ROWS[2]))
+        load_half(mean_k, mean, 1)
+        load_rows(2, range(VECTOR_ROWS[2], PACK))
+        for b in range(1, IMAGES):
             nc.sync.dma_start(out=std_k[b][:], in_=by_k(std, b))
             nc.sync.dma_start(out=mean_k[b][:], in_=by_k(mean, b))
-            if b == 0:
-                nc.sync.dma_start(
-                    out=w_codes_raw[:].bitcast(I32),
-                    in_=out_w_words[0].rearrange("p n t -> p (n t)").bitcast(I32),
-                )
-                for q in range(4):
-                    nc.sync.dma_start(
-                        out=w_plane_raw[32 * q : 32 * q + 4, :].bitcast(I32),
-                        in_=out_w_scales[0, 4 * q : 4 * q + 4, :].bitcast(I32),
-                    )
+            if b + 2 < IMAGES:
+                load_rows(b + 2, range(PACK))
 
         w_codes = consts.tile([P, CHANNELS], U32, align_bytes=64)
         w_plane = consts.tile([P, CHANNELS], U8, align_bytes=64)
@@ -97,100 +109,81 @@ def tile_aattn_pb_t_kernel(tc, content, mean, std, out_w_words, out_w_scales, ou
         )
 
         mu_var = [small.tile([P, PACK, BLOCK_F32], F32, name="mu_var%d" % b) for b in range(IMAGES)]
-        total = [None] * IMAGES
-        squares = [None] * IMAGES
+        parts = [small.tile([P, PACK, BN_CHUNKS, BN_DIM], F32, name="parts%d" % b) for b in range(IMAGES)]
+        total = [small.tile([P, PACK], F32, name="total%d" % b) for b in range(IMAGES)]
+        squares = [small.tile([P, PACK], F32, name="squares%d" % b) for b in range(IMAGES)]
         spread = [small.tile([P, PACK], F32, name="spread%d" % b) for b in range(IMAGES)]
         rstd = [small.tile([P, PACK], F32, name="rstd%d" % b) for b in range(IMAGES)]
         shift = [small.tile([P, PACK], F32, name="shift%d" % b) for b in range(IMAGES)]
-        work = [None] * IMAGES
 
-        def vector_rows(b):
-            return max(0, min(PACK, VECTOR_ROWS - b * PACK))
-
-        def stats_on_vector(b):
-            parts = small.tile([P, PACK, BN_CHUNKS, BN_DIM], F32, name="parts%d" % b)
-            for t in range(vector_rows(b)):
+        def stats_on_vector(b, rows):
+            for t in rows:
                 for c in range(BN_CHUNKS):
                     nc.vector.bn_stats(
-                        out=parts[:, t, c, :], in_=x_k[b][:, t, c * BN_CHUNK : (c + 1) * BN_CHUNK]
+                        out=parts[b][:, t, c, :], in_=x_k[b][:, t, c * BN_CHUNK : (c + 1) * BN_CHUNK]
                     )
                 nc.vector.bn_aggr(
-                    out=mu_var[b][:, t, 0:2], in_=parts[:, t].rearrange("p c s -> p (c s)")
+                    out=mu_var[b][:, t, 0:2], in_=parts[b][:, t].rearrange("p c s -> p (c s)")
                 )
 
-        def means_on_scalar(b):
-            first = vector_rows(b)
-            if first < PACK:
-                total[b] = small.tile([P, PACK], F32, name="total%d" % b)
+        def stats_on_scalar(b):
+            first = VECTOR_ROWS[b]
             for t in range(first, PACK):
                 copy_unread = unread.tile([P, PIXELS], BF16, tag="unread")
                 nc.scalar.activation(
                     out=copy_unread[:], in_=x_k[b][:, t, :], func=ACT.Identity,
                     accum_out=total[b][:, t : t + 1],
                 )
-            if first < PACK:
-                nc.scalar.mul(out=mu_var[b][:, first:, 0], in_=total[b][:, first:], mul=1.0 / PIXELS)
-
-        def spreads_on_scalar(b):
-            first = vector_rows(b)
-            if first < PACK:
-                squares[b] = small.tile([P, PACK], F32, name="squares%d" % b)
+            nc.scalar.mul(out=mu_var[b][:, first:, 0], in_=total[b][:, first:], mul=1.0 / PIXELS)
             for t in range(first, PACK):
                 square_unread = unread.tile([P, PIXELS], BF16, tag="unread")
                 nc.scalar.activation(
                     out=square_unread[:], in_=x_k[b][:, t, :], func=ACT.Square,
                     scale=-1.0, bias=mu_var[b][:, t, 0:1], accum_out=squares[b][:, t : t + 1],
                 )
-            if first < PACK:
-                nc.scalar.mul(out=mu_var[b][:, first:, 1], in_=squares[b][:, first:], mul=1.0 / PIXELS)
+            nc.scalar.mul(out=mu_var[b][:, first:, 1], in_=squares[b][:, first:], mul=1.0 / PIXELS)
+
+        def scale_and_shift(b):
             nc.scalar.activation(
                 out=spread[b][:], in_=mu_var[b][:, :, 1], func=ACT.Sqrt,
                 scale=PIXELS / (PIXELS - 1.0), bias=eps[:],
             )
-
-        def normalise(b):
             nc.vector.reciprocal(out=rstd[b][:], in_=spread[b][:])
             nc.vector.scalar_tensor_tensor(
                 out=shift[b][:], in0=mu_var[b][:, :, 0], scalar=-1.0, in1=rstd[b][:],
                 op0=ALU.mult, op1=ALU.mult,
             )
-            work[b] = normed.tile([P, PACK, PIXELS], F32, name="work", tag="work")
-            for h in range(HALVES):
-                cols = pixels_of(h)
-                for t in range(PACK):
-                    nc.scalar.activation(
-                        out=work[b][:, t, cols], in_=x_k[b][:, t, cols], func=ACT.Identity,
-                        scale=rstd[b][:, t : t + 1], bias=shift[b][:, t : t + 1],
-                    )
 
+        work = [None] * UNITS
         grouped = [None] * UNITS
         banks = [None] * UNITS
+        product = consts.tile([P, PACK, N_TILE], F32)
 
-        def gpsimd_pixels(u):
-            return GPSIMD_PIXELS if u > 0 else 0
-
-        def multiply_by_std_on_vector(u):
-            b, cols = u // HALVES, pixels_of(u, 0, N_TILE - gpsimd_pixels(u))
-            nc.vector.tensor_tensor(
-                out=work[b][:, :, cols], in0=work[b][:, :, cols], in1=std_k[b][:, :, cols],
-                op=ALU.mult,
-            )
-
-        def multiply_by_std_on_gpsimd(u):
-            b, count = u // HALVES, gpsimd_pixels(u)
-            if count > 0:
-                last = pixels_of(u, N_TILE - count, count)
-                nc.gpsimd.tensor_tensor(
-                    out=work[b][:, :, pixels_of(u, 0, count)], in0=work[b][:, :, last],
-                    in1=std_k[b][:, :, last], op=ALU.mult,
+        def normalise(u):
+            b, cols = u // HALVES, pixels_of(u)
+            work[u] = normed.tile([P, PACK, N_TILE], F32, name="work", tag="work")
+            for t in range(PACK):
+                nc.scalar.activation(
+                    out=work[u][:, t, :], in_=x_k[b][:, t, cols], func=ACT.Identity,
+                    scale=rstd[b][:, t : t + 1], bias=shift[b][:, t : t + 1],
                 )
 
-        def add_mean(u, first, count, product_first):
-            b = u // HALVES
+        def vector_pixels(u):
+            return N_TILE - GPSIMD_PIXELS if u > 0 else N_TILE
+
+        def multiply_by_std(engine, u, first, count):
+            if count > 0:
+                engine.tensor_tensor(
+                    out=product[:, :, first : first + count], in0=work[u][:, :, first : first + count],
+                    in1=std_k[u // HALVES][:, :, pixels_of(u, first, count)], op=ALU.mult,
+                )
+
+        def add_mean(u):
+            grouped[u] = quant.tile([P, N_TILE, PACK], BF16, align_bytes=64, name="grouped", tag="grouped")
             nc.vector.tensor_tensor(
-                out=grouped[u][:, first : first + count, :].rearrange("p (c i) t -> p c t i", i=RUN),
-                in0=work[b][:, :, pixels_of(u, product_first, count)].rearrange("p t (c i) -> p c t i", i=RUN),
-                in1=mean_k[b][:, :, pixels_of(u, first, count)].rearrange("p t (c i) -> p c t i", i=RUN),
+                out=grouped[u][:].rearrange("p (c i) t -> p c t i", i=RUN),
+                in0=product[:].rearrange("p t (c i) -> p c t i", i=RUN),
+                in1=mean_k[u // HALVES][:, :, pixels_of(u)].rearrange("p t (c i) -> p c t i", i=RUN),
                 op=ALU.add,
             )
 
@@ -203,13 +196,13 @@ def tile_aattn_pb_t_kernel(tc, content, mean, std, out_w_words, out_w_scales, ou
                 in_=grouped[u][:].rearrange("p n t -> p (n t)"),
             )
             banks[u] = []
-            for m in range(M_TILES):
-                m_cols = slice(m * P, (m + 1) * P)
+            for t in range(PACK):
+                t_cols = slice(t * P, (t + 1) * P)
                 acc = psum.tile([P, N_TILE], F32, tag="acc")
                 nc.tensor.matmul_mx(
                     out=acc[:],
-                    lhsT=w_codes[:, m_cols].bitcast(FP8X4),
-                    lhsT_scale=w_plane[:, m_cols],
+                    lhsT=w_codes[:, t_cols].bitcast(FP8X4),
+                    lhsT_scale=w_plane[:, t_cols],
                     rhs=o_codes[:].bitcast(FP8X4),
                     rhs_scale=o_plane[:],
                     start=True,
@@ -219,40 +212,42 @@ def tile_aattn_pb_t_kernel(tc, content, mean, std, out_w_words, out_w_scales, ou
 
         def add_residual_and_store(u):
             b, cols = u // HALVES, pixels_of(u)
-            for m in range(M_TILES):
+            for t in range(PACK):
                 result = results.tile([P, N_TILE], F32)
                 nc.vector.scalar_tensor_tensor(
-                    out=result[:], in0=banks[u][m][:], scalar=bias[:, m : m + 1],
-                    in1=x_k[b][:, m, cols], op0=ALU.add, op1=ALU.add,
+                    out=result[:], in0=banks[u][t][:], scalar=bias[:, t : t + 1],
+                    in1=x_k[b][:, t, cols], op0=ALU.add, op1=ALU.add,
                 )
-                nc.sync.dma_start(out=by_k(out, b)[:, m, cols], in_=result[:])
+                nc.sync.dma_start(out=by_k(out, b)[:, t, cols], in_=result[:])
 
-        stats_on_vector(0)
-        spreads_on_scalar(0)
+        stats_on_vector(0, range(VECTOR_ROWS[0]))
+        stats_on_scalar(0)
+        stats_on_vector(1, range(1))
+        scale_and_shift(0)
         normalise(0)
-        stats_on_vector(1)
-        means_on_scalar(1)
-        spreads_on_scalar(1)
-        means_on_scalar(2)
+        stats_on_vector(1, range(1, VECTOR_ROWS[1]))
+        normalise(1)
+        stats_on_scalar(1)
+        multiply_by_std(nc.vector, 0, 0, N_TILE)
 
-        multiply_by_std_on_vector(0)
         for u in range(UNITS):
             b = u // HALVES
-            if u % HALVES == HALVES - 1 and b + 1 < IMAGES:
-                normalise(b + 1)
-                if b + 2 < IMAGES:
-                    spreads_on_scalar(b + 2)
-                if b + 3 < IMAGES:
-                    means_on_scalar(b + 3)
-            grouped[u] = quant.tile([P, N_TILE, PACK], BF16, align_bytes=64, name="grouped", tag="grouped")
-            own = N_TILE - gpsimd_pixels(u)
-            add_mean(u, 0, own, 0)
-            multiply_by_std_on_gpsimd(u)
+            add_mean(u)
+            if u + 1 < UNITS:
+                own = vector_pixels(u + 1)
+                multiply_by_std(nc.gpsimd, u + 1, own, N_TILE - own)
             if u >= 1:
                 add_residual_and_store(u - 1)
-            if own < N_TILE:
-                add_mean(u, own, N_TILE - own, 0)
+            if u % HALVES == 0:
+                if b + 2 < IMAGES:
+                    stats_on_vector(b + 2, range(VECTOR_ROWS[b + 2]))
+                if b + 1 < IMAGES:
+                    scale_and_shift(b + 1)
+                    normalise(u + 2)
+                    normalise(u + 3)
+                if b + 2 < IMAGES:
+                    stats_on_scalar(b + 2)
             if u + 1 < UNITS:
-                multiply_by_std_on_vector(u + 1)
+                multiply_by_std(nc.vector, u + 1, 0, vector_pixels(u + 1))
             quantise_and_project(u)
         add_residual_and_store(UNITS - 1)

@@ -27,7 +27,8 @@ BLOCK_F32 = 8
 
 FLOPS = 2 * CHANNELS * CHANNELS * IMAGES * PIXELS
 
-VECTOR_ROWS = (3, 2, 2, 1)
+VECTOR_ROWS = (3, 2, 2, 0)
+EARLY_ROWS = 1
 RUN = 4
 GPSIMD_PIXELS = 224
 
@@ -55,7 +56,7 @@ def tile_aattn_pb_t_kernel(tc, content, mean, std, out_w_words, out_w_scales, ou
         eps = consts.tile([P, 1], F32)
         nc.vector.memset(eps[:], EPS)
         warm = consts.tile([P, 1], F32)
-        nc.scalar.activation(out=warm[:], in_=eps[:], func=ACT.Sqrt)
+        nc.scalar.activation(out=warm[:], in_=eps[:], func=ACT.Abs_reciprocal_sqrt)
         bias = consts.tile([P, PACK], BF16)
         nc.scalar.dma_start(out=bias[:], in_=out_b.rearrange("(j t) -> j t", t=PACK))
         w_plane_raw = consts.tile([P, CHANNELS], U8, align_bytes=64)
@@ -112,7 +113,7 @@ def tile_aattn_pb_t_kernel(tc, content, mean, std, out_w_words, out_w_scales, ou
         parts = [small.tile([P, PACK, BN_CHUNKS, BN_DIM], F32, name="parts%d" % b) for b in range(IMAGES)]
         total = [small.tile([P, PACK], F32, name="total%d" % b) for b in range(IMAGES)]
         squares = [small.tile([P, PACK], F32, name="squares%d" % b) for b in range(IMAGES)]
-        spread = [small.tile([P, PACK], F32, name="spread%d" % b) for b in range(IMAGES)]
+        neg_rstd = [small.tile([P, PACK], F32, name="neg_rstd%d" % b) for b in range(IMAGES)]
         rstd = [small.tile([P, PACK], F32, name="rstd%d" % b) for b in range(IMAGES)]
         shift = [small.tile([P, PACK], F32, name="shift%d" % b) for b in range(IMAGES)]
 
@@ -126,33 +127,33 @@ def tile_aattn_pb_t_kernel(tc, content, mean, std, out_w_words, out_w_scales, ou
                     out=mu_var[b][:, t, 0:2], in_=parts[b][:, t].rearrange("p c s -> p (c s)")
                 )
 
-        def stats_on_scalar(b):
-            first = VECTOR_ROWS[b]
-            for t in range(first, PACK):
+        def stats_on_scalar(b, first, end):
+            for t in range(first, end):
                 copy_unread = unread.tile([P, PIXELS], BF16, tag="unread")
                 nc.scalar.activation(
                     out=copy_unread[:], in_=x_k[b][:, t, :], func=ACT.Identity,
                     accum_out=total[b][:, t : t + 1],
                 )
-            nc.scalar.mul(out=mu_var[b][:, first:, 0], in_=total[b][:, first:], mul=1.0 / PIXELS)
-            for t in range(first, PACK):
+            nc.scalar.mul(out=mu_var[b][:, first:end, 0], in_=total[b][:, first:end], mul=1.0 / PIXELS)
+            for t in range(first, end):
                 square_unread = unread.tile([P, PIXELS], BF16, tag="unread")
                 nc.scalar.activation(
                     out=square_unread[:], in_=x_k[b][:, t, :], func=ACT.Square,
                     scale=-1.0, bias=mu_var[b][:, t, 0:1], accum_out=squares[b][:, t : t + 1],
                 )
-            nc.scalar.mul(out=mu_var[b][:, first:, 1], in_=squares[b][:, first:], mul=1.0 / PIXELS)
+            nc.scalar.mul(out=mu_var[b][:, first:end, 1], in_=squares[b][:, first:end], mul=1.0 / PIXELS)
 
         def scale_and_shift(b):
             nc.scalar.activation(
-                out=spread[b][:], in_=mu_var[b][:, :, 1], func=ACT.Sqrt,
+                out=rstd[b][:], in_=mu_var[b][:, :, 1], func=ACT.Abs_reciprocal_sqrt,
                 scale=PIXELS / (PIXELS - 1.0), bias=eps[:],
             )
-            nc.vector.reciprocal(out=rstd[b][:], in_=spread[b][:])
-            nc.vector.scalar_tensor_tensor(
-                out=shift[b][:], in0=mu_var[b][:, :, 0], scalar=-1.0, in1=rstd[b][:],
-                op0=ALU.mult, op1=ALU.mult,
-            )
+            nc.scalar.mul(out=neg_rstd[b][:], in_=rstd[b][:], mul=-1.0)
+            for t in range(PACK):
+                nc.scalar.activation(
+                    out=shift[b][:, t : t + 1], in_=mu_var[b][:, t, 0:1], func=ACT.Identity,
+                    scale=neg_rstd[b][:, t : t + 1],
+                )
 
         work = [None] * UNITS
         grouped = [None] * UNITS
@@ -210,9 +211,9 @@ def tile_aattn_pb_t_kernel(tc, content, mean, std, out_w_words, out_w_scales, ou
                 )
                 banks[u].append(acc)
 
-        def add_residual_and_store(u):
+        def add_residual_and_store(u, slots):
             b, cols = u // HALVES, pixels_of(u)
-            for t in range(PACK):
+            for t in slots:
                 result = results.tile([P, N_TILE], F32)
                 nc.vector.scalar_tensor_tensor(
                     out=result[:], in0=banks[u][t][:], scalar=bias[:, t : t + 1],
@@ -221,13 +222,13 @@ def tile_aattn_pb_t_kernel(tc, content, mean, std, out_w_words, out_w_scales, ou
                 nc.sync.dma_start(out=by_k(out, b)[:, t, cols], in_=result[:])
 
         stats_on_vector(0, range(VECTOR_ROWS[0]))
-        stats_on_scalar(0)
+        stats_on_scalar(0, VECTOR_ROWS[0], PACK)
         stats_on_vector(1, range(1))
         scale_and_shift(0)
         normalise(0)
         stats_on_vector(1, range(1, VECTOR_ROWS[1]))
         normalise(1)
-        stats_on_scalar(1)
+        stats_on_scalar(1, VECTOR_ROWS[1], PACK)
         multiply_by_std(nc.vector, 0, 0, N_TILE)
 
         for u in range(UNITS):
@@ -236,8 +237,12 @@ def tile_aattn_pb_t_kernel(tc, content, mean, std, out_w_words, out_w_scales, ou
             if u + 1 < UNITS:
                 own = vector_pixels(u + 1)
                 multiply_by_std(nc.gpsimd, u + 1, own, N_TILE - own)
-            if u >= 1:
-                add_residual_and_store(u - 1)
+            if u == UNITS - 1:
+                add_residual_and_store(u - 1, range(1))
+                quantise_and_project(u)
+                add_residual_and_store(u - 1, range(1, PACK))
+            elif u >= 1:
+                add_residual_and_store(u - 1, range(PACK))
             if u % HALVES == 0:
                 if b + 2 < IMAGES:
                     stats_on_vector(b + 2, range(VECTOR_ROWS[b + 2]))
@@ -245,9 +250,12 @@ def tile_aattn_pb_t_kernel(tc, content, mean, std, out_w_words, out_w_scales, ou
                     scale_and_shift(b + 1)
                     normalise(u + 2)
                     normalise(u + 3)
-                if b + 2 < IMAGES:
-                    stats_on_scalar(b + 2)
+                if b + 2 < IMAGES - 1:
+                    stats_on_scalar(b + 2, VECTOR_ROWS[b + 2], PACK)
+                    stats_on_scalar(IMAGES - 1, PACK - EARLY_ROWS, PACK)
+                if b + 2 == IMAGES - 1:
+                    stats_on_scalar(b + 2, VECTOR_ROWS[b + 2], PACK - EARLY_ROWS)
             if u + 1 < UNITS:
                 multiply_by_std(nc.vector, u + 1, 0, vector_pixels(u + 1))
-            quantise_and_project(u)
-        add_residual_and_store(UNITS - 1)
+                quantise_and_project(u)
+        add_residual_and_store(UNITS - 1, range(PACK))

@@ -1,6 +1,7 @@
 from contextlib import ExitStack
 
 import concourse.mybir as mybir
+from concourse.masks import make_identity
 
 F32 = mybir.dt.float32
 BF16 = mybir.dt.bfloat16
@@ -30,7 +31,8 @@ FLOPS = 2 * CHANNELS * CHANNELS * IMAGES * PIXELS
 VECTOR_ROWS = (3, 2, 2, 0)
 EARLY_ROWS = 1
 RUN = 4
-GPSIMD_PIXELS = 224
+GPSIMD_PIXELS = 320
+BANK_PIXELS = 128
 
 
 def tile_aattn_pb_t_kernel(tc, content, mean, std, out_w_words, out_w_scales, out_b, out):
@@ -43,7 +45,8 @@ def tile_aattn_pb_t_kernel(tc, content, mean, std, out_w_words, out_w_scales, ou
         normed = stack.enter_context(tc.tile_pool(name="normed", bufs=3))
         quant = stack.enter_context(tc.tile_pool(name="quant", bufs=2))
         results = stack.enter_context(tc.tile_pool(name="results", bufs=16))
-        psum = stack.enter_context(tc.psum_pool(name="psum", bufs=8))
+        psum = stack.enter_context(tc.psum_pool(name="psum", bufs=6))
+        psum_mean = stack.enter_context(tc.psum_pool(name="psum_mean", bufs=1))
         stack.enter_context(tc.manual_schedule())
 
         def by_k(x, b):
@@ -61,6 +64,8 @@ def tile_aattn_pb_t_kernel(tc, content, mean, std, out_w_words, out_w_scales, ou
         nc.scalar.dma_start(out=bias[:], in_=out_b.rearrange("(j t) -> j t", t=PACK))
         w_plane_raw = consts.tile([P, CHANNELS], U8, align_bytes=64)
         nc.vector.memset(w_plane_raw[:].bitcast(I32), 0)
+        ident = consts.tile([P, P], BF16)
+        make_identity(nc, ident[:])
 
         x_k = [inputs.tile([P, PACK, PIXELS], BF16, name="x_k%d" % b) for b in range(IMAGES)]
         std_k = [inputs.tile([P, PACK, PIXELS], BF16, name="std_k%d" % b) for b in range(IMAGES)]
@@ -158,6 +163,7 @@ def tile_aattn_pb_t_kernel(tc, content, mean, std, out_w_words, out_w_scales, ou
         work = [None] * UNITS
         grouped = [None] * UNITS
         banks = [None] * UNITS
+        mean_banks = [None] * UNITS
         product = consts.tile([P, PACK, N_TILE], F32)
 
         def normalise(u):
@@ -179,14 +185,31 @@ def tile_aattn_pb_t_kernel(tc, content, mean, std, out_w_words, out_w_scales, ou
                     in1=std_k[u // HALVES][:, :, pixels_of(u, first, count)], op=ALU.mult,
                 )
 
-        def add_mean(u):
-            grouped[u] = quant.tile([P, N_TILE, PACK], BF16, align_bytes=64, name="grouped", tag="grouped")
+        def own_pieces():
+            own = N_TILE - GPSIMD_PIXELS
+            return [(first, min(BANK_PIXELS, own - first)) for first in range(0, own, BANK_PIXELS)]
+
+        def mean_to_psum(u):
+            mean_banks[u] = []
+            for k, (first, count) in enumerate(own_pieces()):
+                bank = psum_mean.tile([P, PACK, count], F32, name="mean_bank%d" % k)
+                for t in range(PACK):
+                    nc.tensor.matmul(
+                        out=bank[:, t, :], lhsT=ident[:],
+                        rhs=mean_k[u // HALVES][:, t, pixels_of(u, first, count)], start=True, stop=True,
+                    )
+                mean_banks[u].append(bank)
+
+        def add_mean(u, first, count, mean_part):
             nc.vector.tensor_tensor(
-                out=grouped[u][:].rearrange("p (c i) t -> p c t i", i=RUN),
-                in0=product[:].rearrange("p t (c i) -> p c t i", i=RUN),
-                in1=mean_k[u // HALVES][:, :, pixels_of(u)].rearrange("p t (c i) -> p c t i", i=RUN),
+                out=grouped[u][:, first : first + count, :].rearrange("p (c i) t -> p c t i", i=RUN),
+                in0=mean_part.rearrange("p t (c i) -> p c t i", i=RUN),
+                in1=product[:, :, first : first + count].rearrange("p t (c i) -> p c t i", i=RUN),
                 op=ALU.add,
             )
+
+        def mean_in_sbuf(u, first, count):
+            return mean_k[u // HALVES][:, :, pixels_of(u, first, count)]
 
         def quantise_and_project(u):
             o_codes = quant.tile([P, N_TILE], U32, align_bytes=64)
@@ -230,13 +253,21 @@ def tile_aattn_pb_t_kernel(tc, content, mean, std, out_w_words, out_w_scales, ou
         normalise(1)
         stats_on_scalar(1, VECTOR_ROWS[1], PACK)
         multiply_by_std(nc.vector, 0, 0, N_TILE)
+        mean_to_psum(0)
 
         for u in range(UNITS):
             b = u // HALVES
-            add_mean(u)
+            grouped[u] = quant.tile([P, N_TILE, PACK], BF16, align_bytes=64, name="grouped", tag="grouped")
             if u + 1 < UNITS:
-                own = vector_pixels(u + 1)
-                multiply_by_std(nc.gpsimd, u + 1, own, N_TILE - own)
+                own = N_TILE - GPSIMD_PIXELS
+                add_mean(u, own, GPSIMD_PIXELS, mean_in_sbuf(u, own, GPSIMD_PIXELS))
+                multiply_by_std(nc.gpsimd, u + 1, own, GPSIMD_PIXELS)
+                for (first, count), bank in zip(own_pieces(), mean_banks[u]):
+                    add_mean(u, first, count, bank[:])
+                if u + 2 < UNITS:
+                    mean_to_psum(u + 1)
+            else:
+                add_mean(u, 0, N_TILE, mean_in_sbuf(u, 0, N_TILE))
             if u == UNITS - 1:
                 add_residual_and_store(u - 1, range(1))
                 quantise_and_project(u)

@@ -116,9 +116,8 @@ def tile_aattn_pb_t_kernel(tc, content, mean, std, out_w_words, out_w_scales, ou
 
         mu_var = [small.tile([P, PACK, BLOCK_F32], F32, name="mu_var%d" % b) for b in range(IMAGES)]
         parts = [small.tile([P, PACK, BN_CHUNKS, BN_DIM], F32, name="parts%d" % b) for b in range(IMAGES)]
-        total = [small.tile([P, PACK], F32, name="total%d" % b) for b in range(IMAGES)]
+        neg_mu = [small.tile([P, PACK], F32, name="neg_mu%d" % b) for b in range(IMAGES)]
         squares = [small.tile([P, PACK], F32, name="squares%d" % b) for b in range(IMAGES)]
-        neg_rstd = [small.tile([P, PACK], F32, name="neg_rstd%d" % b) for b in range(IMAGES)]
         rstd = [small.tile([P, PACK], F32, name="rstd%d" % b) for b in range(IMAGES)]
         shift = [small.tile([P, PACK], F32, name="shift%d" % b) for b in range(IMAGES)]
 
@@ -137,27 +136,31 @@ def tile_aattn_pb_t_kernel(tc, content, mean, std, out_w_words, out_w_scales, ou
                 copy_unread = unread.tile([P, PIXELS], BF16, tag="unread")
                 nc.scalar.activation(
                     out=copy_unread[:], in_=x_k[b][:, t, :], func=ACT.Identity,
-                    accum_out=total[b][:, t : t + 1],
+                    scale=-1.0 / PIXELS, accum_out=neg_mu[b][:, t : t + 1],
                 )
-            nc.scalar.mul(out=mu_var[b][:, first:end, 0], in_=total[b][:, first:end], mul=1.0 / PIXELS)
             for t in range(first, end):
                 square_unread = unread.tile([P, PIXELS], BF16, tag="unread")
                 nc.scalar.activation(
                     out=square_unread[:], in_=x_k[b][:, t, :], func=ACT.Square,
-                    scale=-1.0, bias=mu_var[b][:, t, 0:1], accum_out=squares[b][:, t : t + 1],
+                    bias=neg_mu[b][:, t : t + 1], accum_out=squares[b][:, t : t + 1],
                 )
-            nc.scalar.mul(out=mu_var[b][:, first:end, 1], in_=squares[b][:, first:end], mul=1.0 / PIXELS)
 
         def scale_and_shift(b):
+            split = VECTOR_ROWS[b]
+            if split > 0:
+                nc.scalar.mul(out=neg_mu[b][:, 0:split], in_=mu_var[b][:, 0:split, 0], mul=-1.0)
+                nc.scalar.activation(
+                    out=rstd[b][:, 0:split], in_=mu_var[b][:, 0:split, 1], func=ACT.Abs_reciprocal_sqrt,
+                    scale=PIXELS / (PIXELS - 1.0), bias=eps[:],
+                )
             nc.scalar.activation(
-                out=rstd[b][:], in_=mu_var[b][:, :, 1], func=ACT.Abs_reciprocal_sqrt,
-                scale=PIXELS / (PIXELS - 1.0), bias=eps[:],
+                out=rstd[b][:, split:], in_=squares[b][:, split:], func=ACT.Abs_reciprocal_sqrt,
+                scale=1.0 / (PIXELS - 1.0), bias=eps[:],
             )
-            nc.scalar.mul(out=neg_rstd[b][:], in_=rstd[b][:], mul=-1.0)
             for t in range(PACK):
                 nc.scalar.activation(
-                    out=shift[b][:, t : t + 1], in_=mu_var[b][:, t, 0:1], func=ACT.Identity,
-                    scale=neg_rstd[b][:, t : t + 1],
+                    out=shift[b][:, t : t + 1], in_=neg_mu[b][:, t : t + 1], func=ACT.Identity,
+                    scale=rstd[b][:, t : t + 1],
                 )
 
         work = [None] * UNITS

@@ -131,13 +131,17 @@ def tile_aattn_pb_t_kernel(tc, content, mean, std, out_w_words, out_w_scales, ou
                     out=mu_var[b][:, t, 0:2], in_=parts[b][:, t].rearrange("p c s -> p (c s)")
                 )
 
-        def stats_on_scalar(b, first, end):
+        def stats_on_scalar(b, first, end, with_vector_rows):
+            if with_vector_rows:
+                rstd_of_vector_rows(b)
             for t in range(first, end):
                 copy_unread = unread.tile([P, PIXELS], BF16, tag="unread")
                 nc.scalar.activation(
                     out=copy_unread[:], in_=x_k[b][:, t, :], func=ACT.Identity,
                     scale=-1.0 / PIXELS, accum_out=neg_mu[b][:, t : t + 1],
                 )
+            if with_vector_rows:
+                shifts(b, range(VECTOR_ROWS[b]))
             for t in range(first, end):
                 square_unread = unread.tile([P, PIXELS], BF16, tag="unread")
                 nc.scalar.activation(
@@ -145,7 +149,7 @@ def tile_aattn_pb_t_kernel(tc, content, mean, std, out_w_words, out_w_scales, ou
                     bias=neg_mu[b][:, t : t + 1], accum_out=squares[b][:, t : t + 1],
                 )
 
-        def scale_and_shift(b):
+        def rstd_of_vector_rows(b):
             split = VECTOR_ROWS[b]
             if split > 0:
                 nc.scalar.mul(out=neg_mu[b][:, 0:split], in_=mu_var[b][:, 0:split, 0], mul=-1.0)
@@ -153,11 +157,16 @@ def tile_aattn_pb_t_kernel(tc, content, mean, std, out_w_words, out_w_scales, ou
                     out=rstd[b][:, 0:split], in_=mu_var[b][:, 0:split, 1], func=ACT.Abs_reciprocal_sqrt,
                     scale=PIXELS / (PIXELS - 1.0), bias=eps[:],
                 )
+
+        def rstd_of_scalar_rows(b):
+            split = VECTOR_ROWS[b]
             nc.scalar.activation(
                 out=rstd[b][:, split:], in_=squares[b][:, split:], func=ACT.Abs_reciprocal_sqrt,
                 scale=1.0 / (PIXELS - 1.0), bias=eps[:],
             )
-            for t in range(PACK):
+
+        def shifts(b, slots):
+            for t in slots:
                 nc.scalar.activation(
                     out=shift[b][:, t : t + 1], in_=neg_mu[b][:, t : t + 1], func=ACT.Identity,
                     scale=rstd[b][:, t : t + 1],
@@ -169,14 +178,24 @@ def tile_aattn_pb_t_kernel(tc, content, mean, std, out_w_words, out_w_scales, ou
         mean_banks = [None] * UNITS
         product = consts.tile([P, PACK, N_TILE], F32)
 
-        def normalise(u):
+        def normalise(u, slots):
             b, cols = u // HALVES, pixels_of(u)
-            work[u] = normed.tile([P, PACK, N_TILE], F32, name="work", tag="work")
-            for t in range(PACK):
+            if work[u] is None:
+                work[u] = normed.tile([P, PACK, N_TILE], F32, name="work", tag="work")
+            for t in slots:
                 nc.scalar.activation(
                     out=work[u][:, t, :], in_=x_k[b][:, t, cols], func=ACT.Identity,
                     scale=rstd[b][:, t : t + 1], bias=shift[b][:, t : t + 1],
                 )
+
+        def normalise_image(b):
+            first, split = b * HALVES, VECTOR_ROWS[b]
+            normalise(first, range(split))
+            rstd_of_scalar_rows(b)
+            normalise(first + 1, range(split))
+            shifts(b, range(split, PACK))
+            normalise(first, range(split, PACK))
+            normalise(first + 1, range(split, PACK))
 
         def vector_pixels(u):
             return N_TILE - GPSIMD_PIXELS if u > 0 else N_TILE
@@ -248,13 +267,14 @@ def tile_aattn_pb_t_kernel(tc, content, mean, std, out_w_words, out_w_scales, ou
                 nc.sync.dma_start(out=by_k(out, b)[:, t, cols], in_=result[:])
 
         stats_on_vector(0, range(VECTOR_ROWS[0]))
-        stats_on_scalar(0, VECTOR_ROWS[0], PACK)
-        stats_on_vector(1, range(1))
-        scale_and_shift(0)
-        normalise(0)
-        stats_on_vector(1, range(1, VECTOR_ROWS[1]))
-        normalise(1)
-        stats_on_scalar(1, VECTOR_ROWS[1], PACK)
+        stats_on_vector(1, range(VECTOR_ROWS[1]))
+        stats_on_scalar(0, VECTOR_ROWS[0], PACK, False)
+        rstd_of_vector_rows(0)
+        rstd_of_scalar_rows(0)
+        shifts(0, range(PACK))
+        normalise(0, range(PACK))
+        normalise(1, range(PACK))
+        stats_on_scalar(1, VECTOR_ROWS[1], PACK, True)
         multiply_by_std(nc.vector, 0, 0, N_TILE)
         mean_to_psum(0)
 
@@ -281,14 +301,12 @@ def tile_aattn_pb_t_kernel(tc, content, mean, std, out_w_words, out_w_scales, ou
                 if b + 2 < IMAGES:
                     stats_on_vector(b + 2, range(VECTOR_ROWS[b + 2]))
                 if b + 1 < IMAGES:
-                    scale_and_shift(b + 1)
-                    normalise(u + 2)
-                    normalise(u + 3)
+                    normalise_image(b + 1)
                 if b + 2 < IMAGES - 1:
-                    stats_on_scalar(b + 2, VECTOR_ROWS[b + 2], PACK)
-                    stats_on_scalar(IMAGES - 1, PACK - EARLY_ROWS, PACK)
+                    stats_on_scalar(b + 2, VECTOR_ROWS[b + 2], PACK, True)
+                    stats_on_scalar(IMAGES - 1, PACK - EARLY_ROWS, PACK, False)
                 if b + 2 == IMAGES - 1:
-                    stats_on_scalar(b + 2, VECTOR_ROWS[b + 2], PACK - EARLY_ROWS)
+                    stats_on_scalar(b + 2, VECTOR_ROWS[b + 2], PACK - EARLY_ROWS, True)
             if u + 1 < UNITS:
                 multiply_by_std(nc.vector, u + 1, 0, vector_pixels(u + 1))
                 quantise_and_project(u)

@@ -31,7 +31,8 @@ FLOPS = 2 * CHANNELS * CHANNELS * IMAGES * PIXELS
 VECTOR_ROWS = (3, 2, 2, 0)
 EARLY_ROWS = 1
 RUN = 4
-GPSIMD_PIXELS = 320
+GPSIMD_PIXELS = 224
+PSUM_PIXELS = 192
 BANK_PIXELS = 128
 
 
@@ -208,7 +209,7 @@ def tile_aattn_pb_t_kernel(tc, content, mean, std, out_w_words, out_w_scales, ou
                 )
 
         def own_pieces():
-            own = N_TILE - GPSIMD_PIXELS
+            own = PSUM_PIXELS
             return [(first, min(BANK_PIXELS, own - first)) for first in range(0, own, BANK_PIXELS)]
 
         def mean_to_psum(u):
@@ -282,9 +283,8 @@ def tile_aattn_pb_t_kernel(tc, content, mean, std, out_w_words, out_w_scales, ou
             b = u // HALVES
             grouped[u] = quant.tile([P, N_TILE, PACK], BF16, align_bytes=64, name="grouped", tag="grouped")
             if u + 1 < UNITS:
-                own = N_TILE - GPSIMD_PIXELS
-                add_mean(u, own, GPSIMD_PIXELS, mean_in_sbuf(u, own, GPSIMD_PIXELS))
-                multiply_by_std(nc.gpsimd, u + 1, own, GPSIMD_PIXELS)
+                add_mean(u, PSUM_PIXELS, N_TILE - PSUM_PIXELS, mean_in_sbuf(u, PSUM_PIXELS, N_TILE - PSUM_PIXELS))
+                multiply_by_std(nc.gpsimd, u + 1, N_TILE - GPSIMD_PIXELS, GPSIMD_PIXELS)
                 for (first, count), bank in zip(own_pieces(), mean_banks[u]):
                     add_mean(u, first, count, bank[:])
                 if u + 2 < UNITS:

@@ -28,10 +28,11 @@ BLOCK_F32 = 8
 
 FLOPS = 2 * CHANNELS * CHANNELS * IMAGES * PIXELS
 
-VECTOR_ROWS = (3, 2, 2, 0)
+VECTOR_ROWS = (3, 2, 1, 0)
 EARLY_ROWS = 1
 RUN = 4
-GPSIMD_PIXELS = 224
+GPSIMD_PIXELS = 296
+GPSIMD_PIXELS_UNIT_1 = 160
 PSUM_PIXELS = 192
 BANK_PIXELS = 128
 
@@ -123,14 +124,23 @@ def tile_aattn_pb_t_kernel(tc, content, mean, std, out_w_words, out_w_scales, ou
         shift = [small.tile([P, PACK], F32, name="shift%d" % b) for b in range(IMAGES)]
 
         def stats_on_vector(b, rows):
+            waiting = []
             for t in rows:
                 for c in range(BN_CHUNKS):
                     nc.vector.bn_stats(
                         out=parts[b][:, t, c, :], in_=x_k[b][:, t, c * BN_CHUNK : (c + 1) * BN_CHUNK]
                     )
-                nc.vector.bn_aggr(
-                    out=mu_var[b][:, t, 0:2], in_=parts[b][:, t].rearrange("p c s -> p (c s)")
-                )
+                    for row in waiting:
+                        aggregate(b, row)
+                    waiting.clear()
+                waiting.append(t)
+            for row in waiting:
+                aggregate(b, row)
+
+        def aggregate(b, t):
+            nc.vector.bn_aggr(
+                out=mu_var[b][:, t, 0:2], in_=parts[b][:, t].rearrange("p c s -> p (c s)")
+            )
 
         def stats_on_scalar(b, first, end, with_vector_rows):
             if with_vector_rows:
@@ -199,7 +209,7 @@ def tile_aattn_pb_t_kernel(tc, content, mean, std, out_w_words, out_w_scales, ou
             normalise(first + 1, range(split, PACK))
 
         def vector_pixels(u):
-            return N_TILE - GPSIMD_PIXELS if u > 0 else N_TILE
+            return N_TILE - (0, GPSIMD_PIXELS_UNIT_1, GPSIMD_PIXELS)[min(u, 2)]
 
         def multiply_by_std(engine, u, first, count):
             if count > 0:
@@ -273,7 +283,12 @@ def tile_aattn_pb_t_kernel(tc, content, mean, std, out_w_words, out_w_scales, ou
         rstd_of_vector_rows(0)
         rstd_of_scalar_rows(0)
         shifts(0, range(PACK))
-        normalise(0, range(PACK))
+        normalise(0, range(PACK - 1))
+        nc.vector.tensor_scalar(
+            out=work[0][:, PACK - 1, :], in0=x_k[0][:, PACK - 1, pixels_of(0)],
+            scalar1=rstd[0][:, PACK - 1 : PACK], scalar2=shift[0][:, PACK - 1 : PACK],
+            op0=ALU.mult, op1=ALU.add,
+        )
         normalise(1, range(PACK))
         stats_on_scalar(1, VECTOR_ROWS[1], PACK, True)
         multiply_by_std(nc.vector, 0, 0, N_TILE)
@@ -284,7 +299,7 @@ def tile_aattn_pb_t_kernel(tc, content, mean, std, out_w_words, out_w_scales, ou
             grouped[u] = quant.tile([P, N_TILE, PACK], BF16, align_bytes=64, name="grouped", tag="grouped")
             if u + 1 < UNITS:
                 add_mean(u, PSUM_PIXELS, N_TILE - PSUM_PIXELS, mean_in_sbuf(u, PSUM_PIXELS, N_TILE - PSUM_PIXELS))
-                multiply_by_std(nc.gpsimd, u + 1, N_TILE - GPSIMD_PIXELS, GPSIMD_PIXELS)
+                multiply_by_std(nc.gpsimd, u + 1, vector_pixels(u + 1), N_TILE - vector_pixels(u + 1))
                 for (first, count), bank in zip(own_pieces(), mean_banks[u]):
                     add_mean(u, first, count, bank[:])
                 if u + 2 < UNITS:

@@ -30,7 +30,7 @@ FLOPS = 2 * CHANNELS * CHANNELS * IMAGES * PIXELS
 
 VECTOR_ROWS = (3, 2, 1, 0)
 EARLY_ROWS = 1
-RUN = 4
+RUN = 8
 GPSIMD_PIXELS = 296
 GPSIMD_PIXELS_UNIT_1 = 160
 PSUM_PIXELS = 192

@@ -29,7 +29,7 @@ BLOCK_F32 = 8
 FLOPS = 2 * CHANNELS * CHANNELS * IMAGES * PIXELS
 
 VECTOR_ROWS = (3, 2, 1, 0)
-EARLY_ROWS = 1
+EARLY_ROWS = 0
 RUN = 8
 GPSIMD_PIXELS = 296
 GPSIMD_PIXELS_UNIT_1 = 160

@@ -28,13 +28,15 @@ BLOCK_F32 = 8
 
 FLOPS = 2 * CHANNELS * CHANNELS * IMAGES * PIXELS
 
-VECTOR_ROWS = (3, 2, 1, 0)
+VECTOR_ROWS = (3, 2, 2, 0)
 EARLY_ROWS = 0
 RUN = 8
-GPSIMD_PIXELS = 296
-GPSIMD_PIXELS_UNIT_1 = 160
-PSUM_PIXELS = 192
+GPSIMD_PIXELS_SUMS = 96
+GPSIMD_PIXELS_RESIDUAL = 264
+GPSIMD_PIXELS_ROW = 128
+PSUM_PIXELS = 232
 BANK_PIXELS = 128
+RING_SLOTS = 3
 
 
 def tile_aattn_pb_t_kernel(tc, content, mean, std, out_w_words, out_w_scales, out_b, out):
@@ -46,6 +48,7 @@ def tile_aattn_pb_t_kernel(tc, content, mean, std, out_w_words, out_w_scales, ou
         unread = stack.enter_context(tc.tile_pool(name="unread", bufs=4))
         normed = stack.enter_context(tc.tile_pool(name="normed", bufs=3))
         quant = stack.enter_context(tc.tile_pool(name="quant", bufs=2))
+        ring = stack.enter_context(tc.tile_pool(name="ring", bufs=1))
         results = stack.enter_context(tc.tile_pool(name="results", bufs=16))
         psum = stack.enter_context(tc.psum_pool(name="psum", bufs=6))
         psum_mean = stack.enter_context(tc.psum_pool(name="psum_mean", bufs=1))
@@ -187,12 +190,21 @@ def tile_aattn_pb_t_kernel(tc, content, mean, std, out_w_words, out_w_scales, ou
         grouped = [None] * UNITS
         banks = [None] * UNITS
         mean_banks = [None] * UNITS
-        product = consts.tile([P, PACK, N_TILE], F32)
+        products = [None] * UNITS
+        ring_taken = [0]
+
+        def ring_tile(shape, dtype):
+            slot = ring_taken[0] % RING_SLOTS
+            ring_taken[0] = ring_taken[0] + 1
+            return ring.tile(shape, dtype, align_bytes=64, name="ring%d" % slot, tag="ring%d" % slot)
 
         def normalise(u, slots):
             b, cols = u // HALVES, pixels_of(u)
             if work[u] is None:
-                work[u] = normed.tile([P, PACK, N_TILE], F32, name="work", tag="work")
+                if u == 0:
+                    work[u] = ring_tile([P, PACK, N_TILE], F32)
+                else:
+                    work[u] = normed.tile([P, PACK, N_TILE], F32, name="work", tag="work")
             for t in slots:
                 nc.scalar.activation(
                     out=work[u][:, t, :], in_=x_k[b][:, t, cols], func=ACT.Identity,
@@ -208,13 +220,22 @@ def tile_aattn_pb_t_kernel(tc, content, mean, std, out_w_words, out_w_scales, ou
             normalise(first, range(split, PACK))
             normalise(first + 1, range(split, PACK))
 
+        def rows_in_step(u):
+            later = u // HALVES + 2
+            return VECTOR_ROWS[later] if u % HALVES == 0 and later < IMAGES else 0
+
         def vector_pixels(u):
-            return N_TILE - (0, GPSIMD_PIXELS_UNIT_1, GPSIMD_PIXELS)[min(u, 2)]
+            if u == 0:
+                return N_TILE
+            share = GPSIMD_PIXELS_SUMS + GPSIMD_PIXELS_ROW * rows_in_step(u - 1)
+            if u >= 2:
+                share += GPSIMD_PIXELS_RESIDUAL
+            return max(N_TILE - share, 0)
 
         def multiply_by_std(engine, u, first, count):
             if count > 0:
                 engine.tensor_tensor(
-                    out=product[:, :, first : first + count], in0=work[u][:, :, first : first + count],
+                    out=products[u][:, :, first : first + count], in0=work[u][:, :, first : first + count],
                     in1=std_k[u // HALVES][:, :, pixels_of(u, first, count)], op=ALU.mult,
                 )
 
@@ -237,7 +258,7 @@ def tile_aattn_pb_t_kernel(tc, content, mean, std, out_w_words, out_w_scales, ou
             nc.vector.tensor_tensor(
                 out=grouped[u][:, first : first + count, :].rearrange("p (c i) t -> p c t i", i=RUN),
                 in0=mean_part.rearrange("p t (c i) -> p c t i", i=RUN),
-                in1=product[:, :, first : first + count].rearrange("p t (c i) -> p c t i", i=RUN),
+                in1=products[u][:, :, first : first + count].rearrange("p t (c i) -> p c t i", i=RUN),
                 op=ALU.add,
             )
 
@@ -291,14 +312,16 @@ def tile_aattn_pb_t_kernel(tc, content, mean, std, out_w_words, out_w_scales, ou
         )
         normalise(1, range(PACK))
         stats_on_scalar(1, VECTOR_ROWS[1], PACK, True)
+        products[0] = ring_tile([P, PACK, N_TILE], F32)
         multiply_by_std(nc.vector, 0, 0, N_TILE)
         mean_to_psum(0)
 
         for u in range(UNITS):
             b = u // HALVES
-            grouped[u] = quant.tile([P, N_TILE, PACK], BF16, align_bytes=64, name="grouped", tag="grouped")
+            grouped[u] = ring_tile([P, N_TILE, PACK], BF16)
             if u + 1 < UNITS:
                 add_mean(u, PSUM_PIXELS, N_TILE - PSUM_PIXELS, mean_in_sbuf(u, PSUM_PIXELS, N_TILE - PSUM_PIXELS))
+                products[u + 1] = ring_tile([P, PACK, N_TILE], F32)
                 multiply_by_std(nc.gpsimd, u + 1, vector_pixels(u + 1), N_TILE - vector_pixels(u + 1))
                 for (first, count), bank in zip(own_pieces(), mean_banks[u]):
                     add_mean(u, first, count, bank[:])

@@ -162,6 +162,8 @@ def tile_aattn_pb_t_kernel(tc, content, mean, std, out_w_words, out_w_scales, ou
                     out=square_unread[:], in_=x_k[b][:, t, :], func=ACT.Square,
                     bias=neg_mu[b][:, t : t + 1], accum_out=squares[b][:, t : t + 1],
                 )
+                small_instructions(b)
+                waiting[b].append(("rstd", t))
 
         def rstd_of_vector_rows(b):
             split = VECTOR_ROWS[b]
@@ -172,12 +174,20 @@ def tile_aattn_pb_t_kernel(tc, content, mean, std, out_w_words, out_w_scales, ou
                     scale=PIXELS / (PIXELS - 1.0), bias=eps[:],
                 )
 
-        def rstd_of_scalar_rows(b):
-            split = VECTOR_ROWS[b]
-            nc.scalar.activation(
-                out=rstd[b][:, split:], in_=squares[b][:, split:], func=ACT.Abs_reciprocal_sqrt,
-                scale=1.0 / (PIXELS - 1.0), bias=eps[:],
-            )
+        waiting = [[] for b in range(IMAGES)]
+
+        def small_instructions(b):
+            due = list(waiting[b])
+            waiting[b].clear()
+            for kind, t in due:
+                if kind == "rstd":
+                    nc.scalar.activation(
+                        out=rstd[b][:, t : t + 1], in_=squares[b][:, t : t + 1], func=ACT.Abs_reciprocal_sqrt,
+                        scale=1.0 / (PIXELS - 1.0), bias=eps[:],
+                    )
+                    waiting[b].append(("shift", t))
+                else:
+                    shifts(b, [t])
 
         def shifts(b, slots):
             for t in slots:
@@ -212,13 +222,11 @@ def tile_aattn_pb_t_kernel(tc, content, mean, std, out_w_words, out_w_scales, ou
                 )
 
         def normalise_image(b):
-            first, split = b * HALVES, VECTOR_ROWS[b]
-            normalise(first, range(split))
-            rstd_of_scalar_rows(b)
-            normalise(first + 1, range(split))
-            shifts(b, range(split, PACK))
-            normalise(first, range(split, PACK))
-            normalise(first + 1, range(split, PACK))
+            first = b * HALVES
+            for t in range(PACK):
+                normalise(first, [t])
+                small_instructions(b)
+            normalise(first + 1, range(PACK))
 
         def rows_in_step(u):
             later = u // HALVES + 2
@@ -302,9 +310,12 @@ def tile_aattn_pb_t_kernel(tc, content, mean, std, out_w_words, out_w_scales, ou
         stats_on_vector(1, range(VECTOR_ROWS[1]))
         stats_on_scalar(0, VECTOR_ROWS[0], PACK, False)
         rstd_of_vector_rows(0)
-        rstd_of_scalar_rows(0)
-        shifts(0, range(PACK))
-        normalise(0, range(PACK - 1))
+        small_instructions(0)
+        shifts(0, range(2))
+        normalise(0, [0])
+        shifts(0, [2])
+        small_instructions(0)
+        normalise(0, range(1, PACK - 1))
         nc.vector.tensor_scalar(
             out=work[0][:, PACK - 1, :], in0=x_k[0][:, PACK - 1, pixels_of(0)],
             scalar1=rstd[0][:, PACK - 1 : PACK], scalar2=shift[0][:, PACK - 1 : PACK],

@@ -32,7 +32,7 @@ VECTOR_ROWS = (3, 2, 2, 0)
 EARLY_ROWS = 0
 RUN = 8
 GPSIMD_PIXELS_SUMS = 96
-GPSIMD_PIXELS_RESIDUAL = 264
+GPSIMD_PIXELS_RESIDUAL = 280
 GPSIMD_PIXELS_ROW = 128
 PSUM_PIXELS = 232
 BANK_PIXELS = 128

@@ -35,7 +35,7 @@ GPSIMD_PIXELS_SUMS = 96
 GPSIMD_PIXELS_RESIDUAL = 280
 GPSIMD_PIXELS_ROW = 128
 PSUM_PIXELS = 232
-BANK_PIXELS = 128
+BANK_PIXELS = 256
 RING_SLOTS = 3
 
 
@@ -254,7 +254,7 @@ def tile_aattn_pb_t_kernel(tc, content, mean, std, out_w_words, out_w_scales, ou
         def mean_to_psum(u):
             mean_banks[u] = []
             for k, (first, count) in enumerate(own_pieces()):
-                bank = psum_mean.tile([P, PACK, count], F32, name="mean_bank%d" % k)
+                bank = psum_mean.tile([P, PACK, count], BF16, name="mean_bank%d" % k)
                 for t in range(PACK):
                     nc.tensor.matmul(
                         out=bank[:, t, :], lhsT=ident[:],

from contextlib import ExitStack

import concourse.mybir as mybir
from concourse.masks import make_identity

F32 = mybir.dt.float32
BF16 = mybir.dt.bfloat16
I32 = mybir.dt.int32
U32 = mybir.dt.uint32
U8 = mybir.dt.uint8
FP8X4 = mybir.dt.float8_e4m3fn_x4
ALU = mybir.AluOpType
ACT = mybir.ActivationFunctionType

IMAGES = 4
CHANNELS = 512
PIXELS = 1024
EPS = 1e-5
P = 128
PACK = 4
N_TILE = 512
HALVES = PIXELS // N_TILE
UNITS = IMAGES * HALVES
BN_CHUNK = 512
BN_CHUNKS = PIXELS // BN_CHUNK
BN_DIM = 6
BLOCK_F32 = 8

FLOPS = 2 * CHANNELS * CHANNELS * IMAGES * PIXELS

VECTOR_ROWS = (3, 2, 2, 0)
EARLY_ROWS = 0
RUN = 8
GPSIMD_PIXELS_SUMS = 96
GPSIMD_PIXELS_RESIDUAL = 280
GPSIMD_PIXELS_ROW = 128
PSUM_PIXELS = 232
BANK_PIXELS = 256
RING_SLOTS = 3


def tile_aattn_pb_t_kernel(tc, content, mean, std, out_w_words, out_w_scales, out_b, out):
    nc = tc.nc
    with ExitStack() as stack:
        consts = stack.enter_context(tc.tile_pool(name="consts", bufs=1))
        inputs = stack.enter_context(tc.tile_pool(name="inputs", bufs=1))
        small = stack.enter_context(tc.tile_pool(name="small", bufs=1))
        unread = stack.enter_context(tc.tile_pool(name="unread", bufs=4))
        normed = stack.enter_context(tc.tile_pool(name="normed", bufs=3))
        quant = stack.enter_context(tc.tile_pool(name="quant", bufs=2))
        ring = stack.enter_context(tc.tile_pool(name="ring", bufs=1))
        results = stack.enter_context(tc.tile_pool(name="results", bufs=16))
        psum = stack.enter_context(tc.psum_pool(name="psum", bufs=6))
        psum_mean = stack.enter_context(tc.psum_pool(name="psum_mean", bufs=1))
        stack.enter_context(tc.manual_schedule())

        def by_k(x, b):
            return x[b].rearrange("(p t) h w -> p t (h w)", t=PACK)

        def pixels_of(u, first=0, count=N_TILE):
            start = (u % HALVES) * N_TILE + first
            return slice(start, start + count)

        eps = consts.tile([P, 1], F32)
        nc.vector.memset(eps[:], EPS)
        warm = consts.tile([P, 1], F32)
        nc.scalar.activation(out=warm[:], in_=eps[:], func=ACT.Abs_reciprocal_sqrt)
        bias = consts.tile([P, PACK], BF16)
        nc.scalar.dma_start(out=bias[:], in_=out_b.rearrange("(j t) -> j t", t=PACK))
        w_plane_raw = consts.tile([P, CHANNELS], U8, align_bytes=64)
        nc.vector.memset(w_plane_raw[:].bitcast(I32), 0)
        ident = consts.tile([P, P], BF16)
        make_identity(nc, ident[:])

        x_k = [inputs.tile([P, PACK, PIXELS], BF16, name="x_k%d" % b) for b in range(IMAGES)]
        std_k = [inputs.tile([P, PACK, PIXELS], BF16, name="std_k%d" % b) for b in range(IMAGES)]
        mean_k = [inputs.tile([P, PACK, PIXELS], BF16, name="mean_k%d" % b) for b in range(IMAGES)]
        w_codes_raw = consts.tile([P, CHANNELS], U32, align_bytes=64)

        def load_rows(b, rows):
            for t in rows:
                nc.sync.dma_start(out=x_k[b][:, t, :], in_=by_k(content, b)[:, t, :])

        def load_half(tiles, x, u):
            b, cols = u // HALVES, pixels_of(u)
            nc.sync.dma_start(out=tiles[b][:, :, cols], in_=by_k(x, b)[:, :, cols])

        load_rows(0, range(PACK))
        nc.sync.dma_start(
            out=w_codes_raw[:].bitcast(I32),
            in_=out_w_words[0].rearrange("p n t -> p (n t)").bitcast(I32),
        )
        for q in range(4):
            nc.sync.dma_start(
                out=w_plane_raw[32 * q : 32 * q + 4, :].bitcast(I32),
                in_=out_w_scales[0, 4 * q : 4 * q + 4, :].bitcast(I32),
            )
        load_rows(1, range(PACK))
        load_half(std_k, std, 0)
        load_half(mean_k, mean, 0)
        load_half(std_k, std, 1)
        load_rows(2, range(VECTOR_ROWS[2]))
        load_half(mean_k, mean, 1)
        load_rows(2, range(VECTOR_ROWS[2], PACK))
        for b in range(1, IMAGES):
            nc.sync.dma_start(out=std_k[b][:], in_=by_k(std, b))
            nc.sync.dma_start(out=mean_k[b][:], in_=by_k(mean, b))
            if b + 2 < IMAGES:
                load_rows(b + 2, range(PACK))

        w_codes = consts.tile([P, CHANNELS], U32, align_bytes=64)
        w_plane = consts.tile([P, CHANNELS], U8, align_bytes=64)
        nc.gpsimd.tensor_copy(
            out=w_codes[:].rearrange("p (t j) -> p t j", t=PACK),
            in_=w_codes_raw[:].rearrange("p (j t) -> p t j", t=PACK),
        )
        nc.gpsimd.tensor_copy(
            out=w_plane[:].rearrange("p (t j) -> p j t", t=PACK),
            in_=w_plane_raw[:].rearrange("p (j t) -> p j t", t=PACK),
        )

        mu_var = [small.tile([P, PACK, BLOCK_F32], F32, name="mu_var%d" % b) for b in range(IMAGES)]
        parts = [small.tile([P, PACK, BN_CHUNKS, BN_DIM], F32, name="parts%d" % b) for b in range(IMAGES)]
        neg_mu = [small.tile([P, PACK], F32, name="neg_mu%d" % b) for b in range(IMAGES)]
        squares = [small.tile([P, PACK], F32, name="squares%d" % b) for b in range(IMAGES)]
        rstd = [small.tile([P, PACK], F32, name="rstd%d" % b) for b in range(IMAGES)]
        shift = [small.tile([P, PACK], F32, name="shift%d" % b) for b in range(IMAGES)]

        def stats_on_vector(b, rows):
            waiting = []
            for t in rows:
                for c in range(BN_CHUNKS):
                    nc.vector.bn_stats(
                        out=parts[b][:, t, c, :], in_=x_k[b][:, t, c * BN_CHUNK : (c + 1) * BN_CHUNK]
                    )
                    for row in waiting:
                        aggregate(b, row)
                    waiting.clear()
                waiting.append(t)
            for row in waiting:
                aggregate(b, row)

        def aggregate(b, t):
            nc.vector.bn_aggr(
                out=mu_var[b][:, t, 0:2], in_=parts[b][:, t].rearrange("p c s -> p (c s)")
            )

        def stats_on_scalar(b, first, end, with_vector_rows):
            if with_vector_rows:
                rstd_of_vector_rows(b)
            for t in range(first, end):
                copy_unread = unread.tile([P, PIXELS], BF16, tag="unread")
                nc.scalar.activation(
                    out=copy_unread[:], in_=x_k[b][:, t, :], func=ACT.Identity,
                    scale=-1.0 / PIXELS, accum_out=neg_mu[b][:, t : t + 1],
                )
            if with_vector_rows:
                shifts(b, range(VECTOR_ROWS[b]))
            for t in range(first, end):
                square_unread = unread.tile([P, PIXELS], BF16, tag="unread")
                nc.scalar.activation(
                    out=square_unread[:], in_=x_k[b][:, t, :], func=ACT.Square,
                    bias=neg_mu[b][:, t : t + 1], accum_out=squares[b][:, t : t + 1],
                )
                small_instructions(b)
                waiting[b].append(("rstd", t))

        def rstd_of_vector_rows(b):
            split = VECTOR_ROWS[b]
            if split > 0:
                nc.scalar.mul(out=neg_mu[b][:, 0:split], in_=mu_var[b][:, 0:split, 0], mul=-1.0)
                nc.scalar.activation(
                    out=rstd[b][:, 0:split], in_=mu_var[b][:, 0:split, 1], func=ACT.Abs_reciprocal_sqrt,
                    scale=PIXELS / (PIXELS - 1.0), bias=eps[:],
                )

        waiting = [[] for b in range(IMAGES)]

        def small_instructions(b):
            due = list(waiting[b])
            waiting[b].clear()
            for kind, t in due:
                if kind == "rstd":
                    nc.scalar.activation(
                        out=rstd[b][:, t : t + 1], in_=squares[b][:, t : t + 1], func=ACT.Abs_reciprocal_sqrt,
                        scale=1.0 / (PIXELS - 1.0), bias=eps[:],
                    )
                    waiting[b].append(("shift", t))
                else:
                    shifts(b, [t])

        def shifts(b, slots):
            for t in slots:
                nc.scalar.activation(
                    out=shift[b][:, t : t + 1], in_=neg_mu[b][:, t : t + 1], func=ACT.Identity,
                    scale=rstd[b][:, t : t + 1],
                )

        work = [None] * UNITS
        grouped = [None] * UNITS
        banks = [None] * UNITS
        mean_banks = [None] * UNITS
        products = [None] * UNITS
        ring_taken = [0]

        def ring_tile(shape, dtype):
            slot = ring_taken[0] % RING_SLOTS
            ring_taken[0] = ring_taken[0] + 1
            return ring.tile(shape, dtype, align_bytes=64, name="ring%d" % slot, tag="ring%d" % slot)

        def normalise(u, slots):
            b, cols = u // HALVES, pixels_of(u)
            if work[u] is None:
                if u == 0:
                    work[u] = ring_tile([P, PACK, N_TILE], F32)
                else:
                    work[u] = normed.tile([P, PACK, N_TILE], F32, name="work", tag="work")
            for t in slots:
                nc.scalar.activation(
                    out=work[u][:, t, :], in_=x_k[b][:, t, cols], func=ACT.Identity,
                    scale=rstd[b][:, t : t + 1], bias=shift[b][:, t : t + 1],
                )

        def normalise_image(b):
            first = b * HALVES
            for t in range(PACK):
                normalise(first, [t])
                small_instructions(b)
            normalise(first + 1, range(PACK))

        def rows_in_step(u):
            later = u // HALVES + 2
            return VECTOR_ROWS[later] if u % HALVES == 0 and later < IMAGES else 0

        def vector_pixels(u):
            if u == 0:
                return N_TILE
            share = GPSIMD_PIXELS_SUMS + GPSIMD_PIXELS_ROW * rows_in_step(u - 1)
            if u >= 2:
                share += GPSIMD_PIXELS_RESIDUAL
            return max(N_TILE - share, 0)

        def multiply_by_std(engine, u, first, count):
            if count > 0:
                engine.tensor_tensor(
                    out=products[u][:, :, first : first + count], in0=work[u][:, :, first : first + count],
                    in1=std_k[u // HALVES][:, :, pixels_of(u, first, count)], op=ALU.mult,
                )

        def own_pieces():
            own = PSUM_PIXELS
            return [(first, min(BANK_PIXELS, own - first)) for first in range(0, own, BANK_PIXELS)]

        def mean_to_psum(u):
            mean_banks[u] = []
            for k, (first, count) in enumerate(own_pieces()):
                bank = psum_mean.tile([P, PACK, count], BF16, name="mean_bank%d" % k)
                for t in range(PACK):
                    nc.tensor.matmul(
                        out=bank[:, t, :], lhsT=ident[:],
                        rhs=mean_k[u // HALVES][:, t, pixels_of(u, first, count)], start=True, stop=True,
                    )
                mean_banks[u].append(bank)

        def add_mean(u, first, count, mean_part):
            nc.vector.tensor_tensor(
                out=grouped[u][:, first : first + count, :].rearrange("p (c i) t -> p c t i", i=RUN),
                in0=mean_part.rearrange("p t (c i) -> p c t i", i=RUN),
                in1=products[u][:, :, first : first + count].rearrange("p t (c i) -> p c t i", i=RUN),
                op=ALU.add,
            )

        def mean_in_sbuf(u, first, count):
            return mean_k[u // HALVES][:, :, pixels_of(u, first, count)]

        def quantise_and_project(u):
            o_codes = quant.tile([P, N_TILE], U32, align_bytes=64)
            o_plane = quant.tile([P, N_TILE], U8, align_bytes=64)
            nc.vector.quantize_mx(
                out=o_codes[:].bitcast(FP8X4),
                scales=o_plane[:],
                in_=grouped[u][:].rearrange("p n t -> p (n t)"),
            )
            banks[u] = []
            for t in range(PACK):
                t_cols = slice(t * P, (t + 1) * P)
                acc = psum.tile([P, N_TILE], F32, tag="acc")
                nc.tensor.matmul_mx(
                    out=acc[:],
                    lhsT=w_codes[:, t_cols].bitcast(FP8X4),
                    lhsT_scale=w_plane[:, t_cols],
                    rhs=o_codes[:].bitcast(FP8X4),
                    rhs_scale=o_plane[:],
                    start=True,
                    stop=True,
                )
                banks[u].append(acc)

        def add_residual_and_store(u, slots):
            b, cols = u // HALVES, pixels_of(u)
            for t in slots:
                result = results.tile([P, N_TILE], F32)
                nc.vector.scalar_tensor_tensor(
                    out=result[:], in0=banks[u][t][:], scalar=bias[:, t : t + 1],
                    in1=x_k[b][:, t, cols], op0=ALU.add, op1=ALU.add,
                )
                nc.sync.dma_start(out=by_k(out, b)[:, t, cols], in_=result[:])

        stats_on_vector(0, range(VECTOR_ROWS[0]))
        stats_on_vector(1, range(VECTOR_ROWS[1]))
        stats_on_scalar(0, VECTOR_ROWS[0], PACK, False)
        rstd_of_vector_rows(0)
        small_instructions(0)
        shifts(0, range(2))
        normalise(0, [0])
        shifts(0, [2])
        small_instructions(0)
        normalise(0, range(1, PACK - 1))
        nc.vector.tensor_scalar(
            out=work[0][:, PACK - 1, :], in0=x_k[0][:, PACK - 1, pixels_of(0)],
            scalar1=rstd[0][:, PACK - 1 : PACK], scalar2=shift[0][:, PACK - 1 : PACK],
            op0=ALU.mult, op1=ALU.add,
        )
        normalise(1, range(PACK))
        stats_on_scalar(1, VECTOR_ROWS[1], PACK, True)
        products[0] = ring_tile([P, PACK, N_TILE], F32)
        multiply_by_std(nc.vector, 0, 0, N_TILE)
        mean_to_psum(0)

        for u in range(UNITS):
            b = u // HALVES
            grouped[u] = ring_tile([P, N_TILE, PACK], BF16)
            if u + 1 < UNITS:
                add_mean(u, PSUM_PIXELS, N_TILE - PSUM_PIXELS, mean_in_sbuf(u, PSUM_PIXELS, N_TILE - PSUM_PIXELS))
                products[u + 1] = ring_tile([P, PACK, N_TILE], F32)
                multiply_by_std(nc.gpsimd, u + 1, vector_pixels(u + 1), N_TILE - vector_pixels(u + 1))
                for (first, count), bank in zip(own_pieces(), mean_banks[u]):
                    add_mean(u, first, count, bank[:])
                if u + 2 < UNITS:
                    mean_to_psum(u + 1)
            else:
                add_mean(u, 0, N_TILE, mean_in_sbuf(u, 0, N_TILE))
            if u == UNITS - 1:
                add_residual_and_store(u - 1, range(1))
                quantise_and_project(u)
                add_residual_and_store(u - 1, range(1, PACK))
            elif u >= 1:
                add_residual_and_store(u - 1, range(PACK))
            if u % HALVES == 0:
                if b + 2 < IMAGES:
                    stats_on_vector(b + 2, range(VECTOR_ROWS[b + 2]))
                if b + 1 < IMAGES:
                    normalise_image(b + 1)
                if b + 2 < IMAGES - 1:
                    stats_on_scalar(b + 2, VECTOR_ROWS[b + 2], PACK, True)
                    stats_on_scalar(IMAGES - 1, PACK - EARLY_ROWS, PACK, False)
                if b + 2 == IMAGES - 1:
                    stats_on_scalar(b + 2, VECTOR_ROWS[b + 2], PACK - EARLY_ROWS, True)
            if u + 1 < UNITS:
                multiply_by_std(nc.vector, u + 1, 0, vector_pixels(u + 1))
                quantise_and_project(u)
        add_residual_and_store(UNITS - 1, range(PACK))
